import numpy as np
import ml_dtypes


def mxq(x, axis, fmt="e4m3"):
    dtype, down = {"e4m3": (ml_dtypes.float8_e4m3fn, 7), "e5m2": (ml_dtypes.float8_e5m2, 14)}[fmt]
    v = np.moveaxis(np.asarray(x, np.float32).astype(ml_dtypes.bfloat16).astype(np.float64), axis, -1)
    blocks = v.reshape(v.shape[:-1] + (-1, 32))
    amax = np.abs(blocks).max(-1, keepdims=True)
    byte = np.maximum(np.where(amax > 0, np.frexp(amax)[1] - 1 + 127, 0) - down, 1)
    scale = np.exp2(byte - 127.0)
    codes = (blocks / scale).astype(np.float32).astype(dtype).astype(np.float64)
    return np.moveaxis((codes * scale).reshape(v.shape), -1, axis)


WIDE = False


def mx_kscale(k):
    if not WIDE:
        return np.ones(k)
    levels = np.array([10, -10, 5, -5, 0])
    a = np.random.permutation(np.resize(levels, k // 512 * 4)).reshape(k // 512, 4)
    idx = np.arange(k)
    return np.exp2(a[idx // 512, idx % 128 // 32])


BF16 = ml_dtypes.bfloat16


def bf(x):
    return np.asarray(x, np.float32).astype(BF16)


def f64(x):
    return np.asarray(x).astype(np.float64)


N, IN_F, HID, OUT_F = 4096, 512, 512, 128


def setup_inputs():
    s = mx_kscale(HID)
    g = 0.1 + 0.9 * np.random.random_sample(N)
    adj = np.random.random_sample((N, N)) * g[:, None] * g[None, :]
    return {"h1": bf(np.random.standard_normal((N, HID)) * s),
            "adj": bf(adj),
            "W2": bf(np.random.standard_normal((OUT_F, HID)) * 0.125 * np.sqrt(N / HID) / s[None, :]),
            "b2": bf(np.random.standard_normal(OUT_F) * 0.1)}


def reference(h1, adj, W2, b2):
    h = (mxq(f64(h1), 1, "e4m3") @ mxq(f64(W2), 1, "e4m3").T) + f64(b2)
    A = f64(adj) + np.eye(N)
    rowsum = A.sum(axis=1)
    r_inv_sqrt = np.power(rowsum, -0.5)
    r_inv_sqrt = np.where(np.isinf(r_inv_sqrt), 0.0, r_inv_sqrt)
    A = r_inv_sqrt[:, None] * A * r_inv_sqrt[None, :]
    return mxq(A, 1, "e4m3") @ mxq(h, 0, "e4m3")

@@ -1,0 +1,238 @@
+from contextlib import ExitStack
+
+import concourse.mybir as mybir
+from concourse.masks import make_identity
+
+F32 = mybir.dt.float32
+BF16 = mybir.dt.bfloat16
+U32 = mybir.dt.uint32
+U8 = mybir.dt.uint8
+FP8X4 = mybir.dt.float8_e4m3fn_x4
+ALU = mybir.AluOpType
+ACT = mybir.ActivationFunctionType
+
+P = 128
+N = 4096
+HID = 512
+OUTF = 128
+G = 512
+NG = N // G
+RB = G // P
+NA = 4
+FLOPS = 2 * N * HID * OUTF + 2 * N * N * OUTF
+
+
+def tile_gcnlayer_pa_t_kernel(tc, h1, adj, W2, b2, out):
+    nc = tc.nc
+    with ExitStack() as ctx:
+        const = ctx.enter_context(tc.tile_pool(name="const", bufs=1))
+        ringp = ctx.enter_context(tc.tile_pool(name="ring", bufs=12))
+        tlp = ctx.enter_context(tc.tile_pool(name="tl", bufs=4))
+        yp = ctx.enter_context(tc.tile_pool(name="y", bufs=3))
+        grpp = ctx.enter_context(tc.tile_pool(name="grp", bufs=3))
+        codep = ctx.enter_context(tc.tile_pool(name="code", bufs=3))
+        small = ctx.enter_context(tc.tile_pool(name="small", bufs=2))
+        dp = ctx.enter_context(tc.tile_pool(name="diag", bufs=4))
+        outp = ctx.enter_context(tc.tile_pool(name="outp", bufs=2))
+        accp = ctx.enter_context(tc.psum_pool(name="acc", bufs=1))
+        tp = ctx.enter_context(tc.psum_pool(name="tp", bufs=4))
+
+        ident_bf = const.tile([P, P], BF16, name="ident_bf")
+        make_identity(nc, ident_bf[:])
+        ident_f = const.tile([P, P], F32, name="ident_f")
+        make_identity(nc, ident_f[:])
+        b2b = const.tile([P, OUTF], BF16, name="b2b")
+        rbc = const.tile([P, N], F32, name="rbc")
+        rc = const.tile([P, N // P], F32, name="rc")
+        hcodes = const.tile([P, NG, OUTF], U32, name="hcodes", align_bytes=64)
+        hscales = const.tile([P, NG, OUTF], U8, name="hscales", align_bytes=64)
+        w2c = const.tile([P, OUTF], U32, name="w2c", align_bytes=64)
+        w2s = const.tile([P, OUTF], U8, name="w2s", align_bytes=64)
+        w2sb = const.tile([P, HID], BF16, name="w2sb")
+        w2g = const.tile([P, OUTF, 4], BF16, name="w2g", align_bytes=64)
+        junkv = const.tile([P, N], BF16, name="junkv")
+        junks = const.tile([P, N], BF16, name="junks")
+
+        def to_codes(srcs):
+            grp = grpp.tile([P, G, 4], BF16, name="grp", align_bytes=64)
+            for hf in range(2):
+                bank = tp.tile([P, 4, 256], BF16, name="bank", tag="tp")
+                for r2 in range(2):
+                    for t in range(4):
+                        nc.tensor.transpose(
+                            bank[:, t, P * r2 : P * r2 + P],
+                            srcs[2 * hf + r2][:, P * t : P * t + P],
+                            ident_bf[:],
+                        )
+                nc.scalar.copy(
+                    out=grp[:, 256 * hf : 256 * hf + 256, :],
+                    in_=bank[:].rearrange("p t i -> p i t"),
+                )
+            codes = codep.tile([P, G], U32, name="codes", align_bytes=64)
+            scl = codep.tile([P, G], U8, name="scl", align_bytes=64)
+            nc.vector.quantize_mx(
+                out=codes[:].bitcast(FP8X4),
+                scales=scl[:],
+                in_=grp[:].rearrange("p i t -> p (i t)"),
+            )
+            return codes, scl
+
+        nc.sync.dma_start(out=w2sb[:], in_=W2[:, :])
+        nc.sync.dma_start(out=b2b[:], in_=b2.partition_broadcast(P))
+        bankw = tp.tile([P, 4, P], BF16, name="bankw", tag="tp")
+        for t in range(4):
+            nc.tensor.transpose(bankw[:, t, :], w2sb[:, P * t : P * t + P], ident_bf[:])
+        nc.scalar.copy(out=w2g[:], in_=bankw[:].rearrange("p t f -> p f t"))
+        nc.vector.quantize_mx(
+            out=w2c[:].bitcast(FP8X4), scales=w2s[:], in_=w2g[:].rearrange("p f t -> p (f t)")
+        )
+
+        def load_group(a):
+            tiles = []
+            for rb in range(RB):
+                rt = ringp.tile([P, N], BF16, name="rt")
+                b = RB * a + rb
+                nc.sync.dma_start(out=rt[:], in_=adj[P * b : P * b + P, :])
+                tiles.append(rt)
+            return tiles
+
+        def degrees(a, tiles):
+            dv = small.tile([P, 2], F32, name="dv")
+            ds = small.tile([P, 2], F32, name="ds")
+            for rb in range(2):
+                nc.vector.tensor_scalar(
+                    out=junkv[:], in0=tiles[rb][:], scalar1=1.0, scalar2=None,
+                    op0=ALU.mult, op1=ALU.add, accum_out=dv[:, rb : rb + 1],
+                )
+            for rb in range(2):
+                nc.scalar.activation(
+                    out=junks[:], in_=tiles[2 + rb][:], func=ACT.Copy, accum_out=ds[:, rb : rb + 1]
+                )
+            deg = small.tile([P, RB], F32, name="deg")
+            nc.vector.tensor_scalar_add(out=deg[:, 0:2], in0=dv[:], scalar1=1.0)
+            nc.vector.tensor_scalar_add(out=deg[:, 2:4], in0=ds[:], scalar1=1.0)
+            sq = small.tile([P, RB], F32, name="sq")
+            nc.scalar.sqrt(out=sq[:], in_=deg[:])
+            r0 = small.tile([P, RB], F32, name="r0")
+            nc.vector.reciprocal(out=r0[:], in_=sq[:])
+            t1 = small.tile([P, RB], F32, name="t1")
+            nc.vector.tensor_mul(out=t1[:], in0=r0[:], in1=r0[:])
+            t2 = small.tile([P, RB], F32, name="t2")
+            nc.vector.tensor_mul(out=t2[:], in0=t1[:], in1=deg[:])
+            t3 = small.tile([P, RB], F32, name="t3")
+            nc.vector.tensor_scalar(
+                out=t3[:], in0=t2[:], scalar1=-0.5, scalar2=1.5, op0=ALU.mult, op1=ALU.add
+            )
+            nc.vector.tensor_mul(out=rc[:, RB * a : RB * a + RB], in0=r0[:], in1=t3[:])
+            bankf = tp.tile([P, G], F32, name="bankf", tag="tp")
+            for rb in range(RB):
+                nc.tensor.transpose(
+                    bankf[:, P * rb : P * rb + P],
+                    rc[:, RB * a + rb : RB * a + rb + 1].to_broadcast([P, P]),
+                    ident_f[:],
+                )
+            nc.scalar.copy(out=rbc[:, G * a : G * a + G], in_=bankf[:])
+
+        def h_chunk(g):
+            h1t = tlp.tile([P, RB, HID], BF16, name="tl")
+            nc.sync.dma_start(
+                out=h1t[:], in_=h1[G * g : G * g + G, :].rearrange("(t p) k -> p t k", p=P)
+            )
+            codes, scl = to_codes([h1t[:, t, :] for t in range(RB)])
+            hb = tp.tile([P, RB, OUTF], F32, name="hb", tag="tp")
+            for t in range(RB):
+                nc.tensor.matmul_mx(
+                    out=hb[:, t, :],
+                    lhsT=codes[:, P * t : P * t + P].bitcast(FP8X4),
+                    lhsT_scale=scl[:, P * t : P * t + P],
+                    rhs=w2c[:].bitcast(FP8X4),
+                    rhs_scale=w2s[:],
+                    start=True,
+                    stop=True,
+                )
+            hg = outp.tile([P, OUTF, RB], BF16, name="hg", align_bytes=64)
+            nc.vector.tensor_tensor(
+                out=hg[:],
+                in0=hb[:].rearrange("p t f -> p f t"),
+                in1=b2b[:].unsqueeze(2).to_broadcast([P, OUTF, RB]),
+                op=ALU.add,
+            )
+            nc.vector.quantize_mx(
+                out=hcodes[:, g, :].bitcast(FP8X4),
+                scales=hscales[:, g, :],
+                in_=hg[:].rearrange("p f t -> p (f t)"),
+            )
+
+        acc = {}
+        done = {}
+
+        def process(s, g, srcs):
+            y = yp.tile([P, RB, G], BF16, name="y")
+            for rb in range(RB):
+                ri = rc[:, RB * s + rb : RB * s + rb + 1]
+                nc.vector.scalar_tensor_tensor(
+                    out=y[:, rb, :], in0=srcs[rb], scalar=ri, in1=rbc[:, G * g : G * g + G],
+                    op0=ALU.mult, op1=ALU.mult,
+                )
+                if s == g:
+                    d = dp.tile([P, P], F32, name="d")
+                    nc.gpsimd.tensor_tensor(
+                        out=d[:], in0=srcs[rb][:, P * rb : P * rb + P], in1=ident_f[:], op=ALU.add
+                    )
+                    nc.vector.scalar_tensor_tensor(
+                        out=y[:, rb, P * rb : P * rb + P], in0=d[:], scalar=ri,
+                        in1=rbc[:, G * g + P * rb : G * g + P * rb + P],
+                        op0=ALU.mult, op1=ALU.mult,
+                    )
+            codes, scl = to_codes([y[:, rb, :] for rb in range(RB)])
+            if s not in acc:
+                acc[s] = accp.tile([P, G], F32, name="acc%d" % (s % NA), tag="acc%d" % (s % NA))
+                done[s] = 0
+            nc.tensor.matmul_mx(
+                out=acc[s][:],
+                lhsT=hcodes[:, g, :].bitcast(FP8X4),
+                lhsT_scale=hscales[:, g, :],
+                rhs=codes[:].bitcast(FP8X4),
+                rhs_scale=scl[:],
+                start=(done[s] == 0),
+                stop=(done[s] == NG - 1),
+            )
+            done[s] += 1
+            if done[s] == NG:
+                finish(s)
+
+        def finish(s):
+            ot = outp.tile([P, G], F32, name="ot")
+            nc.scalar.copy(out=ot[:], in_=acc[s][:])
+            bo = tp.tile([P, RB, OUTF], F32, name="bo", tag="tp")
+            for rb in range(RB):
+                nc.tensor.transpose(bo[:, rb, :], ot[:, P * rb : P * rb + P], ident_f[:])
+            ob = outp.tile([P, RB, OUTF], F32, name="ob")
+            nc.scalar.copy(out=ob[:], in_=bo[:])
+            nc.sync.dma_start(
+                out=out[G * s : G * s + G, :].rearrange("(r p) f -> p r f", p=P), in_=ob[:]
+            )
+
+        def reread(s, g):
+            tl = tlp.tile([P, RB, G], BF16, name="tl")
+            nc.sync.dma_start(
+                out=tl[:],
+                in_=adj[G * s : G * s + G, G * g : G * g + G].rearrange("(r p) c -> p r c", p=P),
+            )
+            return [tl[:, rb, :] for rb in range(RB)]
+
+        for a in range(NG):
+            tiles = load_group(a)
+            degrees(a, tiles)
+            if a == 0:
+                for g in range(NG):
+                    h_chunk(g)
+            if a < NA:
+                for g in range(a + 1):
+                    process(a, g, [tiles[rb][:, G * g : G * g + G] for rb in range(RB)])
+            for s in range(min(a, NA)):
+                process(s, a, reread(s, a))
+        for s in range(NA, NG):
+            tiles = load_group(s)
+            for g in range(NG):
+                process(s, g, [tiles[rb][:, G * g : G * g + G] for rb in range(RB)])

@@ -18,31 +18,35 @@ OUTF = 128
 G = 512
 NG = N // G
 RB = G // P
-NA = 4
+NV = 3
 FLOPS = 2 * N * HID * OUTF + 2 * N * N * OUTF
+
+
+def scalar_evacuates(b, g):
+    return (b + g) % 3 == 0
 
 
 def tile_gcnlayer_pa_t_kernel(tc, h1, adj, W2, b2, out):
     nc = tc.nc
     with ExitStack() as ctx:
         const = ctx.enter_context(tc.tile_pool(name="const", bufs=1))
-        ringp = ctx.enter_context(tc.tile_pool(name="ring", bufs=12))
-        tlp = ctx.enter_context(tc.tile_pool(name="tl", bufs=4))
-        yp = ctx.enter_context(tc.tile_pool(name="y", bufs=3))
+        ringp = ctx.enter_context(tc.tile_pool(name="ring", bufs=9))
+        xp = ctx.enter_context(tc.tile_pool(name="x", bufs=3))
         grpp = ctx.enter_context(tc.tile_pool(name="grp", bufs=3))
         codep = ctx.enter_context(tc.tile_pool(name="code", bufs=3))
+        hp = ctx.enter_context(tc.tile_pool(name="hp", bufs=2))
         small = ctx.enter_context(tc.tile_pool(name="small", bufs=2))
-        dp = ctx.enter_context(tc.tile_pool(name="diag", bufs=4))
-        outp = ctx.enter_context(tc.tile_pool(name="outp", bufs=2))
-        accp = ctx.enter_context(tc.psum_pool(name="acc", bufs=1))
-        tp = ctx.enter_context(tc.psum_pool(name="tp", bufs=4))
+        dp = ctx.enter_context(tc.tile_pool(name="diag", bufs=2))
+        partp = ctx.enter_context(tc.tile_pool(name="part", bufs=28))
+        outp = ctx.enter_context(tc.tile_pool(name="outp", bufs=3))
+        obp = ctx.enter_context(tc.psum_pool(name="ob", bufs=2))
+        tp = ctx.enter_context(tc.psum_pool(name="tp", bufs=6))
 
         ident_bf = const.tile([P, P], BF16, name="ident_bf")
         make_identity(nc, ident_bf[:])
         ident_f = const.tile([P, P], F32, name="ident_f")
         make_identity(nc, ident_f[:])
         b2b = const.tile([P, OUTF], BF16, name="b2b")
-        rbc = const.tile([P, N], F32, name="rbc")
         rc = const.tile([P, N // P], F32, name="rc")
         hcodes = const.tile([P, NG, OUTF], U32, name="hcodes", align_bytes=64)
         hscales = const.tile([P, NG, OUTF], U8, name="hscales", align_bytes=64)
@@ -52,30 +56,6 @@ def tile_gcnlayer_pa_t_kernel(tc, h1, adj, W2, b2, out):
         w2g = const.tile([P, OUTF, 4], BF16, name="w2g", align_bytes=64)
         junkv = const.tile([P, N], BF16, name="junkv")
         junks = const.tile([P, N], BF16, name="junks")
-
-        def to_codes(srcs):
-            grp = grpp.tile([P, G, 4], BF16, name="grp", align_bytes=64)
-            for hf in range(2):
-                bank = tp.tile([P, 4, 256], BF16, name="bank", tag="tp")
-                for r2 in range(2):
-                    for t in range(4):
-                        nc.tensor.transpose(
-                            bank[:, t, P * r2 : P * r2 + P],
-                            srcs[2 * hf + r2][:, P * t : P * t + P],
-                            ident_bf[:],
-                        )
-                nc.scalar.copy(
-                    out=grp[:, 256 * hf : 256 * hf + 256, :],
-                    in_=bank[:].rearrange("p t i -> p i t"),
-                )
-            codes = codep.tile([P, G], U32, name="codes", align_bytes=64)
-            scl = codep.tile([P, G], U8, name="scl", align_bytes=64)
-            nc.vector.quantize_mx(
-                out=codes[:].bitcast(FP8X4),
-                scales=scl[:],
-                in_=grp[:].rearrange("p i t -> p (i t)"),
-            )
-            return codes, scl
 
         nc.sync.dma_start(out=w2sb[:], in_=W2[:, :])
         nc.sync.dma_start(out=b2b[:], in_=b2.partition_broadcast(P))
@@ -87,30 +67,27 @@ def tile_gcnlayer_pa_t_kernel(tc, h1, adj, W2, b2, out):
             out=w2c[:].bitcast(FP8X4), scales=w2s[:], in_=w2g[:].rearrange("p f t -> p (f t)")
         )
 
-        def load_group(a):
-            tiles = []
-            for rb in range(RB):
-                rt = ringp.tile([P, N], BF16, name="rt")
-                b = RB * a + rb
-                nc.sync.dma_start(out=rt[:], in_=adj[P * b : P * b + P, :])
-                tiles.append(rt)
-            return tiles
+        def load_block(b, c0):
+            rt = ringp.tile([P, N], BF16, name="rt")
+            nc.sync.dma_start(out=rt[:, c0:N], in_=adj[P * b : P * b + P, c0:N])
+            return rt
 
         def degrees(a, tiles):
-            dv = small.tile([P, 2], F32, name="dv")
-            ds = small.tile([P, 2], F32, name="ds")
-            for rb in range(2):
-                nc.vector.tensor_scalar(
-                    out=junkv[:], in0=tiles[rb][:], scalar1=1.0, scalar2=None,
-                    op0=ALU.mult, op1=ALU.add, accum_out=dv[:, rb : rb + 1],
-                )
-            for rb in range(2):
-                nc.scalar.activation(
-                    out=junks[:], in_=tiles[2 + rb][:], func=ACT.Copy, accum_out=ds[:, rb : rb + 1]
-                )
+            dv = small.tile([P, RB], F32, name="dv")
+            ds = small.tile([P, RB], F32, name="ds")
+            for rb in range(RB):
+                if rb < NV:
+                    nc.vector.tensor_scalar(
+                        out=junkv[:], in0=tiles[rb][:], scalar1=1.0, scalar2=None,
+                        op0=ALU.mult, op1=ALU.add, accum_out=dv[:, rb : rb + 1],
+                    )
+                else:
+                    nc.scalar.activation(
+                        out=junks[:], in_=tiles[rb][:], func=ACT.Copy, accum_out=ds[:, rb : rb + 1]
+                    )
             deg = small.tile([P, RB], F32, name="deg")
-            nc.vector.tensor_scalar_add(out=deg[:, 0:2], in0=dv[:], scalar1=1.0)
-            nc.vector.tensor_scalar_add(out=deg[:, 2:4], in0=ds[:], scalar1=1.0)
+            nc.vector.tensor_scalar_add(out=deg[:, 0:NV], in0=dv[:, 0:NV], scalar1=1.0)
+            nc.vector.tensor_scalar_add(out=deg[:, NV:RB], in0=ds[:, NV:RB], scalar1=1.0)
             sq = small.tile([P, RB], F32, name="sq")
             nc.scalar.sqrt(out=sq[:], in_=deg[:])
             r0 = small.tile([P, RB], F32, name="r0")
@@ -124,33 +101,43 @@ def tile_gcnlayer_pa_t_kernel(tc, h1, adj, W2, b2, out):
                 out=t3[:], in0=t2[:], scalar1=-0.5, scalar2=1.5, op0=ALU.mult, op1=ALU.add
             )
             nc.vector.tensor_mul(out=rc[:, RB * a : RB * a + RB], in0=r0[:], in1=t3[:])
-            bankf = tp.tile([P, G], F32, name="bankf", tag="tp")
-            for rb in range(RB):
-                nc.tensor.transpose(
-                    bankf[:, P * rb : P * rb + P],
-                    rc[:, RB * a + rb : RB * a + rb + 1].to_broadcast([P, P]),
-                    ident_f[:],
-                )
-            nc.scalar.copy(out=rbc[:, G * a : G * a + G], in_=bankf[:])
 
         def h_chunk(g):
-            h1t = tlp.tile([P, RB, HID], BF16, name="tl")
+            h1t = hp.tile([P, RB, HID], BF16, name="h1t")
             nc.sync.dma_start(
                 out=h1t[:], in_=h1[G * g : G * g + G, :].rearrange("(t p) k -> p t k", p=P)
             )
-            codes, scl = to_codes([h1t[:, t, :] for t in range(RB)])
+            hgrp = hp.tile([P, G, 4], BF16, name="hgrp", align_bytes=64)
+            for hf in range(2):
+                bank = tp.tile([P, 4, 256], BF16, name="bankh", tag="tp")
+                for r2 in range(2):
+                    for t in range(4):
+                        nc.tensor.transpose(
+                            bank[:, t, P * r2 : P * r2 + P],
+                            h1t[:, 2 * hf + r2, P * t : P * t + P],
+                            ident_bf[:],
+                        )
+                nc.scalar.copy(
+                    out=hgrp[:, 256 * hf : 256 * hf + 256, :],
+                    in_=bank[:].rearrange("p t i -> p i t"),
+                )
+            hc = hp.tile([P, G], U32, name="hc", align_bytes=64)
+            hs = hp.tile([P, G], U8, name="hs", align_bytes=64)
+            nc.vector.quantize_mx(
+                out=hc[:].bitcast(FP8X4), scales=hs[:], in_=hgrp[:].rearrange("p i t -> p (i t)")
+            )
             hb = tp.tile([P, RB, OUTF], F32, name="hb", tag="tp")
             for t in range(RB):
                 nc.tensor.matmul_mx(
                     out=hb[:, t, :],
-                    lhsT=codes[:, P * t : P * t + P].bitcast(FP8X4),
-                    lhsT_scale=scl[:, P * t : P * t + P],
+                    lhsT=hc[:, P * t : P * t + P].bitcast(FP8X4),
+                    lhsT_scale=hs[:, P * t : P * t + P],
                     rhs=w2c[:].bitcast(FP8X4),
                     rhs_scale=w2s[:],
                     start=True,
                     stop=True,
                 )
-            hg = outp.tile([P, OUTF, RB], BF16, name="hg", align_bytes=64)
+            hg = hp.tile([P, OUTF, RB], BF16, name="hg", align_bytes=64)
             nc.vector.tensor_tensor(
                 out=hg[:],
                 in0=hb[:].rearrange("p t f -> p f t"),
@@ -163,76 +150,88 @@ def tile_gcnlayer_pa_t_kernel(tc, h1, adj, W2, b2, out):
                 in_=hg[:].rearrange("p f t -> p (f t)"),
             )
 
-        acc = {}
-        done = {}
+        part = {}
 
-        def process(s, g, srcs):
-            y = yp.tile([P, RB, G], BF16, name="y")
-            for rb in range(RB):
-                ri = rc[:, RB * s + rb : RB * s + rb + 1]
-                nc.vector.scalar_tensor_tensor(
-                    out=y[:, rb, :], in0=srcs[rb], scalar=ri, in1=rbc[:, G * g : G * g + G],
-                    op0=ALU.mult, op1=ALU.mult,
+        def job(b, g0, g1, rt):
+            ri = rc[:, b : b + 1]
+            x = xp.tile([P, N], F32, name="x")
+            nc.gpsimd.tensor_scalar(
+                out=x[:, G * g0 : G * (g1 + 1)], in0=rt[:, G * g0 : G * (g1 + 1)],
+                scalar1=ri, scalar2=0.0, op0=ALU.mult, op1=ALU.add,
+            )
+            if g0 <= b // RB <= g1:
+                d = dp.tile([P, P], F32, name="d")
+                nc.gpsimd.tensor_tensor(
+                    out=d[:], in0=rt[:, P * b : P * b + P], in1=ident_f[:], op=ALU.add
                 )
-                if s == g:
-                    d = dp.tile([P, P], F32, name="d")
-                    nc.gpsimd.tensor_tensor(
-                        out=d[:], in0=srcs[rb][:, P * rb : P * rb + P], in1=ident_f[:], op=ALU.add
+                nc.gpsimd.tensor_scalar(
+                    out=x[:, P * b : P * b + P], in0=d[:],
+                    scalar1=ri, scalar2=0.0, op0=ALU.mult, op1=ALU.add,
+                )
+            grp = grpp.tile([P, NG, P, 4], BF16, name="grp", align_bytes=64)
+            for g in range(g0, g1 + 1):
+                bank = tp.tile([P, 4, P], F32, name="bank", tag="tp")
+                for t in range(4):
+                    c = G * g + P * t
+                    nc.tensor.transpose(bank[:, t, :], x[:, c : c + P], ident_f[:])
+                if scalar_evacuates(b, g):
+                    for t in range(4):
+                        nc.scalar.activation(
+                            out=grp[:, g, :, t], in_=bank[:, t, :], func=ACT.Copy,
+                            scale=rc[:, RB * g + t : RB * g + t + 1],
+                        )
+                else:
+                    nc.vector.tensor_tensor(
+                        out=grp[:, g, :, :],
+                        in0=bank[:].rearrange("p t i -> p i t"),
+                        in1=rc[:, RB * g : RB * g + RB].unsqueeze(1).to_broadcast([P, P, RB]),
+                        op=ALU.mult,
                     )
-                    nc.vector.scalar_tensor_tensor(
-                        out=y[:, rb, P * rb : P * rb + P], in0=d[:], scalar=ri,
-                        in1=rbc[:, G * g + P * rb : G * g + P * rb + P],
-                        op0=ALU.mult, op1=ALU.mult,
-                    )
-            codes, scl = to_codes([y[:, rb, :] for rb in range(RB)])
-            if s not in acc:
-                acc[s] = accp.tile([P, G], F32, name="acc%d" % (s % NA), tag="acc%d" % (s % NA))
-                done[s] = 0
-            nc.tensor.matmul_mx(
-                out=acc[s][:],
-                lhsT=hcodes[:, g, :].bitcast(FP8X4),
-                lhsT_scale=hscales[:, g, :],
-                rhs=codes[:].bitcast(FP8X4),
-                rhs_scale=scl[:],
-                start=(done[s] == 0),
-                stop=(done[s] == NG - 1),
-            )
-            done[s] += 1
-            if done[s] == NG:
-                finish(s)
-
-        def finish(s):
-            ot = outp.tile([P, G], F32, name="ot")
-            nc.scalar.copy(out=ot[:], in_=acc[s][:])
-            bo = tp.tile([P, RB, OUTF], F32, name="bo", tag="tp")
-            for rb in range(RB):
-                nc.tensor.transpose(bo[:, rb, :], ot[:, P * rb : P * rb + P], ident_f[:])
-            ob = outp.tile([P, RB, OUTF], F32, name="ob")
-            nc.scalar.copy(out=ob[:], in_=bo[:])
-            nc.sync.dma_start(
-                out=out[G * s : G * s + G, :].rearrange("(r p) f -> p r f", p=P), in_=ob[:]
-            )
-
-        def reread(s, g):
-            tl = tlp.tile([P, RB, G], BF16, name="tl")
-            nc.sync.dma_start(
-                out=tl[:],
-                in_=adj[G * s : G * s + G, G * g : G * g + G].rearrange("(r p) c -> p r c", p=P),
-            )
-            return [tl[:, rb, :] for rb in range(RB)]
+            codes = codep.tile([P, NG, P], U32, name="codes", align_bytes=64)
+            scl = codep.tile([P, NG, P], U8, name="scl", align_bytes=64)
+            g = g0
+            while g <= g1:
+                n = 1
+                while 2 * n <= g1 - g + 1:
+                    n = 2 * n
+                nc.vector.quantize_mx(
+                    out=codes[:, g : g + n, :].rearrange("p g i -> p (g i)").bitcast(FP8X4),
+                    scales=scl[:, g : g + n, :].rearrange("p g i -> p (g i)"),
+                    in_=grp[:, g : g + n, :, :].rearrange("p g i t -> p (g i t)"),
+                )
+                g += n
+            ob = obp.tile([P, OUTF], F32, name="ob")
+            for g in range(g0, g1 + 1):
+                nc.tensor.matmul_mx(
+                    out=ob[:],
+                    lhsT=codes[:, g, :].bitcast(FP8X4),
+                    lhsT_scale=scl[:, g, :],
+                    rhs=hcodes[:, g, :].bitcast(FP8X4),
+                    rhs_scale=hscales[:, g, :],
+                    start=(g == g0),
+                    stop=(g == g1),
+                )
+            if g1 < NG - 1:
+                pt = partp.tile([P, OUTF], F32, name="pt")
+                nc.scalar.copy(out=pt[:], in_=ob[:])
+                part[b] = pt
+            else:
+                o = outp.tile([P, OUTF], F32, name="o")
+                if g0 == 0:
+                    nc.scalar.copy(out=o[:], in_=ob[:])
+                else:
+                    nc.vector.tensor_tensor(out=o[:], in0=ob[:], in1=part[b][:], op=ALU.add)
+                nc.sync.dma_start(out=out[P * b : P * b + P, :], in_=o[:])
 
         for a in range(NG):
-            tiles = load_group(a)
+            tiles = [load_block(RB * a + rb, 0) for rb in range(RB)]
             degrees(a, tiles)
             if a == 0:
                 for g in range(NG):
                     h_chunk(g)
-            if a < NA:
-                for g in range(a + 1):
-                    process(a, g, [tiles[rb][:, G * g : G * g + G] for rb in range(RB)])
-            for s in range(min(a, NA)):
-                process(s, a, reread(s, a))
-        for s in range(NA, NG):
-            tiles = load_group(s)
-            for g in range(NG):
-                process(s, g, [tiles[rb][:, G * g : G * g + G] for rb in range(RB)])
+            for rb in range(RB):
+                job(RB * a + rb, 0, a, tiles[rb])
+        for a in range(NG - 1):
+            for rb in range(RB):
+                b = RB * a + rb
+                job(b, a + 1, NG - 1, load_block(b, G * (a + 1)))

@@ -10,52 +10,65 @@ U8 = mybir.dt.uint8
 FP8X4 = mybir.dt.float8_e4m3fn_x4
 ALU = mybir.AluOpType
 ACT = mybir.ActivationFunctionType
+AX = mybir.AxisListType
 
 P = 128
 N = 4096
 HID = 512
 OUTF = 128
-G = 512
-NG = N // G
-RB = G // P
-NV = 3
+Q = 1024
+NG = 8
+PRE = 8
+NS = [4,4,6,6,8,8,10,10]
 FLOPS = 2 * N * HID * OUTF + 2 * N * N * OUTF
-
-
-def scalar_evacuates(b, g):
-    return (b + g) % 3 == 0
 
 
 def tile_gcnlayer_pa_t_kernel(tc, h1, adj, W2, b2, out):
     nc = tc.nc
+    adjq = adj.rearrange("i (t c) -> (i t) c", t=4)
+    h1v = h1.rearrange("(t g p) k -> g p t k", t=4, g=NG)
     with ExitStack() as ctx:
         const = ctx.enter_context(tc.tile_pool(name="const", bufs=1))
-        ringp = ctx.enter_context(tc.tile_pool(name="ring", bufs=9))
-        xp = ctx.enter_context(tc.tile_pool(name="x", bufs=3))
-        grpp = ctx.enter_context(tc.tile_pool(name="grp", bufs=3))
+        ringp = ctx.enter_context(tc.tile_pool(name="ring", bufs=11))
+        yp = ctx.enter_context(tc.tile_pool(name="y", bufs=3))
+        grpp = ctx.enter_context(tc.tile_pool(name="grp", bufs=4))
         codep = ctx.enter_context(tc.tile_pool(name="code", bufs=3))
         hp = ctx.enter_context(tc.tile_pool(name="hp", bufs=2))
         small = ctx.enter_context(tc.tile_pool(name="small", bufs=2))
-        dp = ctx.enter_context(tc.tile_pool(name="diag", bufs=2))
+        dp = ctx.enter_context(tc.tile_pool(name="diag", bufs=12))
         partp = ctx.enter_context(tc.tile_pool(name="part", bufs=28))
-        outp = ctx.enter_context(tc.tile_pool(name="outp", bufs=3))
-        obp = ctx.enter_context(tc.psum_pool(name="ob", bufs=2))
-        tp = ctx.enter_context(tc.psum_pool(name="tp", bufs=6))
+        outp = ctx.enter_context(tc.tile_pool(name="outp", bufs=4))
+        obp = ctx.enter_context(tc.psum_pool(name="ob", bufs=3))
+        tp = ctx.enter_context(tc.psum_pool(name="tp", bufs=5))
+        ctx.enter_context(tc.manual_schedule())
 
         ident_bf = const.tile([P, P], BF16, name="ident_bf")
         make_identity(nc, ident_bf[:])
         ident_f = const.tile([P, P], F32, name="ident_f")
         make_identity(nc, ident_f[:])
+        red = const.tile([P, 32], F32, name="red")
+        nc.vector.tensor_reduce(
+            out=red[:], in_=ident_f[:].rearrange("k (a b) -> k a b", b=4), axis=AX.X, op=ALU.add
+        )
+        b4 = const.tile([P, 32, 4], F32, name="b4")
+        nc.vector.tensor_copy(out=b4[:], in_=red[:].unsqueeze(2).to_broadcast([P, 32, 4]))
+        lt = const.tile([P, 4, 32, 4], F32, name="lt")
+        nc.vector.memset(lt[:], 0.0)
+        for t in range(4):
+            nc.vector.memset(lt[:, t, :, t], 1.0)
+        sel = ident_f[:].rearrange("k (i t) -> k i t", t=4)[:, :, 0]
+        dmask = ident_bf[:].rearrange("k (i t) -> k t i", t=4)
         b2b = const.tile([P, OUTF], BF16, name="b2b")
-        rc = const.tile([P, N // P], F32, name="rc")
-        hcodes = const.tile([P, NG, OUTF], U32, name="hcodes", align_bytes=64)
-        hscales = const.tile([P, NG, OUTF], U8, name="hscales", align_bytes=64)
+        ra = const.tile([P, 4, NG, 4], F32, name="ra")
+        rq = const.tile([P, Q], F32, name="rq")
+        hcodes = [const.tile([P, OUTF], U32, name="hcodes%d" % g, align_bytes=64) for g in range(NG)]
+        hscales = [const.tile([P, OUTF], U8, name="hscales%d" % g, align_bytes=64) for g in range(NG)]
         w2c = const.tile([P, OUTF], U32, name="w2c", align_bytes=64)
         w2s = const.tile([P, OUTF], U8, name="w2s", align_bytes=64)
         w2sb = const.tile([P, HID], BF16, name="w2sb")
         w2g = const.tile([P, OUTF, 4], BF16, name="w2g", align_bytes=64)
-        junkv = const.tile([P, N], BF16, name="junkv")
-        junks = const.tile([P, N], BF16, name="junks")
+        junkv = const.tile([P, Q], BF16, name="junkv")
+        junks = const.tile([P, Q], BF16, name="junks")
 
         nc.sync.dma_start(out=w2sb[:], in_=W2[:, :])
         nc.sync.dma_start(out=b2b[:], in_=b2.partition_broadcast(P))
@@ -67,67 +80,64 @@ def tile_gcnlayer_pa_t_kernel(tc, h1, adj, W2, b2, out):
             out=w2c[:].bitcast(FP8X4), scales=w2s[:], in_=w2g[:].rearrange("p f t -> p (f t)")
         )
 
-        def load_block(b, c0):
-            rt = ringp.tile([P, N], BF16, name="rt")
-            nc.sync.dma_start(out=rt[:, c0:N], in_=adj[P * b : P * b + P, c0:N])
-            return rt
+        jobs = [(NG * t + s, 0, s) for s in range(NG) for t in range(4)]
+        jobs += [(NG * t + s, s + 1, NG - 1) for s in range(NG - 1) for t in range(4)]
+        raw = {}
+        dsub = {}
+        h1t = {}
 
-        def degrees(a, tiles):
-            dv = small.tile([P, RB], F32, name="dv")
-            ds = small.tile([P, RB], F32, name="ds")
-            for rb in range(RB):
-                if rb < NV:
-                    nc.vector.tensor_scalar(
-                        out=junkv[:], in0=tiles[rb][:], scalar1=1.0, scalar2=None,
-                        op0=ALU.mult, op1=ALU.add, accum_out=dv[:, rb : rb + 1],
-                    )
-                else:
-                    nc.scalar.activation(
-                        out=junks[:], in_=tiles[rb][:], func=ACT.Copy, accum_out=ds[:, rb : rb + 1]
-                    )
-            deg = small.tile([P, RB], F32, name="deg")
-            nc.vector.tensor_scalar_add(out=deg[:, 0:NV], in0=dv[:, 0:NV], scalar1=1.0)
-            nc.vector.tensor_scalar_add(out=deg[:, NV:RB], in0=ds[:, NV:RB], scalar1=1.0)
-            sq = small.tile([P, RB], F32, name="sq")
-            nc.scalar.sqrt(out=sq[:], in_=deg[:])
-            r0 = small.tile([P, RB], F32, name="r0")
-            nc.vector.reciprocal(out=r0[:], in_=sq[:])
-            t1 = small.tile([P, RB], F32, name="t1")
-            nc.vector.tensor_mul(out=t1[:], in0=r0[:], in1=r0[:])
-            t2 = small.tile([P, RB], F32, name="t2")
-            nc.vector.tensor_mul(out=t2[:], in0=t1[:], in1=deg[:])
-            t3 = small.tile([P, RB], F32, name="t3")
-            nc.vector.tensor_scalar(
-                out=t3[:], in0=t2[:], scalar1=-0.5, scalar2=1.5, op0=ALU.mult, op1=ALU.add
-            )
-            nc.vector.tensor_mul(out=rc[:, RB * a : RB * a + RB], in0=r0[:], in1=t3[:])
-
-        def h_chunk(g):
-            h1t = hp.tile([P, RB, HID], BF16, name="h1t")
+        def emit_load(n):
+            if n >= len(jobs):
+                return
+            b, g0, g1 = jobs[n]
+            s = b % NG
+            if g0 == 0 and b < NG:
+                h1t[s] = hp.tile([P, 4, HID], BF16, name="h1t", bufs=3)
+                nc.sync.dma_start(out=h1t[s][:], in_=h1v[s])
+            rt = ringp.tile([P, 4, Q], BF16, name="rt")
+            c0 = P * g0
             nc.sync.dma_start(
-                out=h1t[:], in_=h1[G * g : G * g + G, :].rearrange("(t p) k -> p t k", p=P)
+                out=rt[:, :, c0:Q],
+                in_=adjq[4 * P * b : 4 * P * b + 4 * P, c0:Q].rearrange("(m k) c -> k m c", k=P),
             )
-            hgrp = hp.tile([P, G, 4], BF16, name="hgrp", align_bytes=64)
+            raw[n] = rt
+            if g0 == 0:
+                d = dp.tile([P, 4, 32], F32, name="d")
+                for m in range(4):
+                    cd = P * s + 32 * m
+                    nc.gpsimd.tensor_tensor(
+                        out=d[:, m, :], in0=rt[:, m, cd : cd + 32], in1=dmask[:, b // NG, :], op=ALU.add
+                    )
+                dsub[n] = d
+
+        hst = {}
+
+        def h_a(g):
+            hgrp = hp.tile([P, 512, 4], BF16, name="hgrp", align_bytes=64)
             for hf in range(2):
                 bank = tp.tile([P, 4, 256], BF16, name="bankh", tag="tp")
                 for r2 in range(2):
                     for t in range(4):
                         nc.tensor.transpose(
                             bank[:, t, P * r2 : P * r2 + P],
-                            h1t[:, 2 * hf + r2, P * t : P * t + P],
+                            h1t[g][:, 2 * hf + r2, P * t : P * t + P],
                             ident_bf[:],
                         )
                 nc.scalar.copy(
                     out=hgrp[:, 256 * hf : 256 * hf + 256, :],
                     in_=bank[:].rearrange("p t i -> p i t"),
                 )
-            hc = hp.tile([P, G], U32, name="hc", align_bytes=64)
-            hs = hp.tile([P, G], U8, name="hs", align_bytes=64)
+            hst[g] = {"hgrp": hgrp}
+
+        def h_b(g):
+            hgrp = hst[g]["hgrp"]
+            hc = hp.tile([P, 512], U32, name="hc", align_bytes=64)
+            hs = hp.tile([P, 512], U8, name="hs", align_bytes=64)
             nc.vector.quantize_mx(
                 out=hc[:].bitcast(FP8X4), scales=hs[:], in_=hgrp[:].rearrange("p i t -> p (i t)")
             )
-            hb = tp.tile([P, RB, OUTF], F32, name="hb", tag="tp")
-            for t in range(RB):
+            hb = tp.tile([P, 4, OUTF], F32, name="hb", tag="tp")
+            for t in range(4):
                 nc.tensor.matmul_mx(
                     out=hb[:, t, :],
                     lhsT=hc[:, P * t : P * t + P].bitcast(FP8X4),
@@ -137,77 +147,162 @@ def tile_gcnlayer_pa_t_kernel(tc, h1, adj, W2, b2, out):
                     start=True,
                     stop=True,
                 )
-            hg = hp.tile([P, OUTF, RB], BF16, name="hg", align_bytes=64)
+            hst[g]["hb"] = hb
+
+        def h_c(g):
+            hb = hst[g]["hb"]
+            hg = hp.tile([P, OUTF, 4], BF16, name="hg", align_bytes=64)
             nc.vector.tensor_tensor(
                 out=hg[:],
                 in0=hb[:].rearrange("p t f -> p f t"),
-                in1=b2b[:].unsqueeze(2).to_broadcast([P, OUTF, RB]),
+                in1=b2b[:].unsqueeze(2).to_broadcast([P, OUTF, 4]),
                 op=ALU.add,
             )
             nc.vector.quantize_mx(
-                out=hcodes[:, g, :].bitcast(FP8X4),
-                scales=hscales[:, g, :],
+                out=hcodes[g][:].bitcast(FP8X4),
+                scales=hscales[g][:],
                 in_=hg[:].rearrange("p f t -> p (f t)"),
             )
 
+        st = {}
+
+        def sums_begin(s):
+            psv = small.tile([P, 16], F32, name="psv")
+            pss = small.tile([P, 16], F32, name="pss")
+            nc.vector.memset(psv[:], 0.0)
+            nc.vector.memset(pss[:], 0.0)
+            st[s] = {"psv": psv, "pss": pss}
+
+        def sum_v(s, i):
+            nc.vector.tensor_scalar(
+                out=junkv[:], in0=raw[4 * s + i // 4][:, i % 4, :], scalar1=1.0, scalar2=None,
+                op0=ALU.mult, op1=ALU.add, accum_out=st[s]["psv"][:, i : i + 1],
+            )
+
+        def sum_s(s, i):
+            nc.scalar.activation(
+                out=junks[:], in_=raw[4 * s + i // 4][:, i % 4, :], func=ACT.Copy,
+                accum_out=st[s]["pss"][:, i : i + 1],
+            )
+
+        def r_part1(s):
+            dqp = tp.tile([P, 16], F32, name="dqp", tag="tp")
+            b4v = b4[:].rearrange("k a b -> k (a b)")
+            nc.tensor.matmul(out=dqp[:], lhsT=b4v, rhs=st[s]["psv"][:], start=True, stop=False)
+            nc.tensor.matmul(out=dqp[:], lhsT=b4v, rhs=st[s]["pss"][:], start=False, stop=True)
+            deg = small.tile([P, 16], F32, name="deg")
+            nc.vector.tensor_scalar_add(out=deg[:], in0=dqp[:], scalar1=1.0)
+            sq = small.tile([P, 16], F32, name="sq")
+            nc.scalar.sqrt(out=sq[:], in_=deg[:])
+            st[s]["deg"] = deg
+            st[s]["sq"] = sq
+
+        def r_part2(s):
+            deg = st[s]["deg"]
+            r0 = small.tile([P, 16], F32, name="r0")
+            nc.vector.reciprocal(out=r0[:], in_=st[s]["sq"][:])
+            t1 = small.tile([P, 16], F32, name="t1")
+            nc.vector.tensor_mul(out=t1[:], in0=r0[:], in1=r0[:])
+            t2 = small.tile([P, 16], F32, name="t2")
+            nc.vector.tensor_mul(out=t2[:], in0=t1[:], in1=deg[:])
+            t3 = small.tile([P, 16], F32, name="t3")
+            nc.vector.tensor_scalar(
+                out=t3[:], in0=t2[:], scalar1=-0.5, scalar2=1.5, op0=ALU.mult, op1=ALU.add
+            )
+            nc.vector.tensor_mul(
+                out=ra[:, :, s, :],
+                in0=r0[:].rearrange("p (t m) -> p t m", m=4),
+                in1=t3[:].rearrange("p (t m) -> p t m", m=4),
+            )
+            rx = small.tile([P, 4, 4, 32], F32, name="rx")
+            nc.vector.tensor_tensor(
+                out=rx[:],
+                in0=ra[:, :, s, :].unsqueeze(3).to_broadcast([P, 4, 4, 32]),
+                in1=sel.unsqueeze(1).unsqueeze(1).to_broadcast([P, 4, 4, 32]),
+                op=ALU.mult,
+            )
+            bq = tp.tile([P, P], F32, name="bq", tag="tp")
+            for t in range(4):
+                nc.tensor.matmul(
+                    out=bq[:],
+                    lhsT=lt[:, t, :, :].rearrange("k a b -> k (a b)"),
+                    rhs=rx[:, t, :, :].rearrange("k m i -> k (m i)"),
+                    start=(t == 0),
+                    stop=(t == 3),
+                )
+            st[s]["bq"] = bq
+
+        def r_part3(s):
+            nc.vector.tensor_copy(out=rq[:, P * s : P * s + P], in_=st[s]["bq"][:])
+
+        js = {}
         part = {}
 
-        def job(b, g0, g1, rt):
-            ri = rc[:, b : b + 1]
-            x = xp.tile([P, N], F32, name="x")
-            nc.gpsimd.tensor_scalar(
-                out=x[:, G * g0 : G * (g1 + 1)], in0=rt[:, G * g0 : G * (g1 + 1)],
-                scalar1=ri, scalar2=0.0, op0=ALU.mult, op1=ALU.add,
-            )
-            if g0 <= b // RB <= g1:
-                d = dp.tile([P, P], F32, name="d")
-                nc.gpsimd.tensor_tensor(
-                    out=d[:], in0=rt[:, P * b : P * b + P], in1=ident_f[:], op=ALU.add
+        def stage_a(n):
+            b, g0, g1 = jobs[n]
+            s = b % NG
+            t = b // NG
+            y = yp.tile([P, 4, Q], BF16, name="y")
+            c0 = P * g0
+            c1 = P * (g1 + 1)
+            for m in range(4):
+                ri = ra[:, t, s, m : m + 1]
+                nc.vector.scalar_tensor_tensor(
+                    out=y[:, m, c0:c1], in0=raw[n][:, m, c0:c1], scalar=ri, in1=rq[:, c0:c1],
+                    op0=ALU.mult, op1=ALU.mult,
                 )
-                nc.gpsimd.tensor_scalar(
-                    out=x[:, P * b : P * b + P], in0=d[:],
-                    scalar1=ri, scalar2=0.0, op0=ALU.mult, op1=ALU.add,
-                )
-            grp = grpp.tile([P, NG, P, 4], BF16, name="grp", align_bytes=64)
-            for g in range(g0, g1 + 1):
-                bank = tp.tile([P, 4, P], F32, name="bank", tag="tp")
-                for t in range(4):
-                    c = G * g + P * t
-                    nc.tensor.transpose(bank[:, t, :], x[:, c : c + P], ident_f[:])
-                if scalar_evacuates(b, g):
-                    for t in range(4):
-                        nc.scalar.activation(
-                            out=grp[:, g, :, t], in_=bank[:, t, :], func=ACT.Copy,
-                            scale=rc[:, RB * g + t : RB * g + t + 1],
-                        )
-                else:
-                    nc.vector.tensor_tensor(
-                        out=grp[:, g, :, :],
-                        in0=bank[:].rearrange("p t i -> p i t"),
-                        in1=rc[:, RB * g : RB * g + RB].unsqueeze(1).to_broadcast([P, P, RB]),
-                        op=ALU.mult,
+                if g0 == 0:
+                    cd = P * s + 32 * m
+                    nc.vector.scalar_tensor_tensor(
+                        out=y[:, m, cd : cd + 32], in0=dsub[n][:, m, :], scalar=ri,
+                        in1=rq[:, cd : cd + 32], op0=ALU.mult, op1=ALU.mult,
                     )
+            js[n] = {"y": y}
+
+        def stage_b(n, sq):
+            b, g0, g1 = jobs[n]
+            y = js[n]["y"]
+            grp = grpp.tile([P, NG, 512], BF16, name="grp", align_bytes=64)
+            g = g0
+            while g <= g1:
+                k = min(2, g1 - g + 1)
+                bank = tp.tile([P, 2, 512], BF16, name="bank", tag="tp")
+                for gl in range(k):
+                    for m in range(4):
+                        c = P * (g + gl)
+                        nc.tensor.transpose(
+                            bank[:, gl, P * m : P * m + P], y[:, m, c : c + P], ident_bf[:]
+                        )
+                nc.scalar.copy(out=grp[:, g : g + k, :], in_=bank[:, 0:k, :])
+                if sq:
+                    sum_s(*sq.pop(0))
+                g += k
+            js[n]["grp"] = grp
+
+        def stage_c(n):
+            b, g0, g1 = jobs[n]
+            grp = js[n]["grp"]
             codes = codep.tile([P, NG, P], U32, name="codes", align_bytes=64)
             scl = codep.tile([P, NG, P], U8, name="scl", align_bytes=64)
             g = g0
             while g <= g1:
-                n = 1
-                while 2 * n <= g1 - g + 1:
-                    n = 2 * n
+                k = 1
+                while 2 * k <= g1 - g + 1:
+                    k = 2 * k
                 nc.vector.quantize_mx(
-                    out=codes[:, g : g + n, :].rearrange("p g i -> p (g i)").bitcast(FP8X4),
-                    scales=scl[:, g : g + n, :].rearrange("p g i -> p (g i)"),
-                    in_=grp[:, g : g + n, :, :].rearrange("p g i t -> p (g i t)"),
+                    out=codes[:, g : g + k, :].rearrange("p g i -> p (g i)").bitcast(FP8X4),
+                    scales=scl[:, g : g + k, :].rearrange("p g i -> p (g i)"),
+                    in_=grp[:, g : g + k, :].rearrange("p g i -> p (g i)"),
                 )
-                g += n
+                g += k
             ob = obp.tile([P, OUTF], F32, name="ob")
             for g in range(g0, g1 + 1):
                 nc.tensor.matmul_mx(
                     out=ob[:],
                     lhsT=codes[:, g, :].bitcast(FP8X4),
                     lhsT_scale=scl[:, g, :],
-                    rhs=hcodes[:, g, :].bitcast(FP8X4),
-                    rhs_scale=hscales[:, g, :],
+                    rhs=hcodes[g][:].bitcast(FP8X4),
+                    rhs_scale=hscales[g][:],
                     start=(g == g0),
                     stop=(g == g1),
                 )
@@ -216,22 +311,68 @@ def tile_gcnlayer_pa_t_kernel(tc, h1, adj, W2, b2, out):
                 nc.scalar.copy(out=pt[:], in_=ob[:])
                 part[b] = pt
             else:
-                o = outp.tile([P, OUTF], F32, name="o")
                 if g0 == 0:
+                    o = outp.tile([P, OUTF], F32, name="o")
                     nc.scalar.copy(out=o[:], in_=ob[:])
+                    js[n]["o"] = o
                 else:
-                    nc.vector.tensor_tensor(out=o[:], in0=ob[:], in1=part[b][:], op=ALU.add)
-                nc.sync.dma_start(out=out[P * b : P * b + P, :], in_=o[:])
+                    js[n]["ob"] = ob
 
-        for a in range(NG):
-            tiles = [load_block(RB * a + rb, 0) for rb in range(RB)]
-            degrees(a, tiles)
-            if a == 0:
-                for g in range(NG):
-                    h_chunk(g)
-            for rb in range(RB):
-                job(RB * a + rb, 0, a, tiles[rb])
-        for a in range(NG - 1):
-            for rb in range(RB):
-                b = RB * a + rb
-                job(b, a + 1, NG - 1, load_block(b, G * (a + 1)))
+        def stage_d(n):
+            b = jobs[n][0]
+            if "ob" in js[n]:
+                o = outp.tile([P, OUTF], F32, name="o")
+                nc.vector.tensor_tensor(out=o[:], in0=js[n]["ob"][:], in1=part[b][:], op=ALU.add)
+                js[n]["o"] = o
+            if "o" in js[n]:
+                nc.sync.dma_start(out=out[P * b : P * b + P, :], in_=js[n]["o"][:])
+
+        for n in range(PRE):
+            emit_load(n)
+        sums_begin(0)
+        for i in range(16):
+            if i % 4 < 3:
+                sum_v(0, i)
+            else:
+                sum_s(0, i)
+        r_part1(0)
+        r_part2(0)
+        r_part3(0)
+        h_a(0)
+        h_b(0)
+        h_c(0)
+        sq = []
+        nj = len(jobs)
+        for n in range(nj + 3):
+            for q in range(1, NG):
+                if n == max(0, 4 * q - 7):
+                    sums_begin(q)
+                    sq.extend([(q, i) for i in range(NS[q])])
+                if n == 4 * q - 4:
+                    for i in range(NS[q], 16):
+                        sum_v(q, i)
+                if n == 4 * q - 3:
+                    r_part1(q)
+                if n == 4 * q - 2:
+                    r_part2(q)
+                if n == 4 * q - 1:
+                    r_part3(q)
+            if n < nj:
+                stage_a(n)
+                emit_load(n + PRE)
+            if n // 4 + 1 < NG:
+                if n % 4 == 0:
+                    h_a(n // 4 + 1)
+                if n % 4 == 1:
+                    h_b(n // 4 + 1)
+                if n % 4 == 2:
+                    h_c(n // 4 + 1)
+            if 1 <= n <= nj:
+                stage_b(n - 1, sq)
+            if n % 4 == 0:
+                while sq and sq[0][0] <= n // 4 + 1:
+                    sum_s(*sq.pop(0))
+            if 2 <= n <= nj + 1:
+                stage_c(n - 2)
+            if n >= 3:
+                stage_d(n - 3)

@@ -40,7 +40,6 @@ def tile_gcnlayer_pa_t_kernel(tc, h1, adj, W2, b2, out):
         outp = ctx.enter_context(tc.tile_pool(name="outp", bufs=4))
         obp = ctx.enter_context(tc.psum_pool(name="ob", bufs=3))
         tp = ctx.enter_context(tc.psum_pool(name="tp", bufs=5))
-        ctx.enter_context(tc.manual_schedule())
 
         ident_bf = const.tile([P, P], BF16, name="ident_bf")
         make_identity(nc, ident_bf[:])

@@ -19,7 +19,7 @@ OUTF = 128
 Q = 1024
 NG = 8
 PRE = 8
-NS = [4,4,6,6,8,8,10,10]
+NS = [4, 6, 8, 9, 10, 11, 12, 14]
 FLOPS = 2 * N * HID * OUTF + 2 * N * N * OUTF
 
 
@@ -29,13 +29,13 @@ def tile_gcnlayer_pa_t_kernel(tc, h1, adj, W2, b2, out):
     h1v = h1.rearrange("(t g p) k -> g p t k", t=4, g=NG)
     with ExitStack() as ctx:
         const = ctx.enter_context(tc.tile_pool(name="const", bufs=1))
-        ringp = ctx.enter_context(tc.tile_pool(name="ring", bufs=11))
+        ringp = ctx.enter_context(tc.tile_pool(name="ring", bufs=10))
         yp = ctx.enter_context(tc.tile_pool(name="y", bufs=3))
         grpp = ctx.enter_context(tc.tile_pool(name="grp", bufs=4))
         codep = ctx.enter_context(tc.tile_pool(name="code", bufs=3))
         hp = ctx.enter_context(tc.tile_pool(name="hp", bufs=2))
         small = ctx.enter_context(tc.tile_pool(name="small", bufs=2))
-        dp = ctx.enter_context(tc.tile_pool(name="diag", bufs=12))
+        dp = ctx.enter_context(tc.tile_pool(name="diag", bufs=2))
         partp = ctx.enter_context(tc.tile_pool(name="part", bufs=28))
         outp = ctx.enter_context(tc.tile_pool(name="outp", bufs=4))
         obp = ctx.enter_context(tc.psum_pool(name="ob", bufs=3))
@@ -57,6 +57,10 @@ def tile_gcnlayer_pa_t_kernel(tc, h1, adj, W2, b2, out):
             nc.vector.memset(lt[:, t, :, t], 1.0)
         sel = ident_f[:].rearrange("k (i t) -> k i t", t=4)[:, :, 0]
         dmask = ident_bf[:].rearrange("k (i t) -> k t i", t=4)
+        maskd = const.tile([P, 4, 4, P], BF16, name="maskd")
+        nc.vector.memset(maskd[:], 0.0)
+        for m in range(4):
+            nc.vector.tensor_copy(out=maskd[:, :, m, 32 * m : 32 * m + 32], in_=dmask)
         b2b = const.tile([P, OUTF], BF16, name="b2b")
         ra = const.tile([P, 4, NG, 4], F32, name="ra")
         rq = const.tile([P, Q], F32, name="rq")
@@ -82,7 +86,6 @@ def tile_gcnlayer_pa_t_kernel(tc, h1, adj, W2, b2, out):
         jobs = [(NG * t + s, 0, s) for s in range(NG) for t in range(4)]
         jobs += [(NG * t + s, s + 1, NG - 1) for s in range(NG - 1) for t in range(4)]
         raw = {}
-        dsub = {}
         h1t = {}
 
         def emit_load(n):
@@ -100,14 +103,6 @@ def tile_gcnlayer_pa_t_kernel(tc, h1, adj, W2, b2, out):
                 in_=adjq[4 * P * b : 4 * P * b + 4 * P, c0:Q].rearrange("(m k) c -> k m c", k=P),
             )
             raw[n] = rt
-            if g0 == 0:
-                d = dp.tile([P, 4, 32], F32, name="d")
-                for m in range(4):
-                    cd = P * s + 32 * m
-                    nc.gpsimd.tensor_tensor(
-                        out=d[:, m, :], in0=rt[:, m, cd : cd + 32], in1=dmask[:, b // NG, :], op=ALU.add
-                    )
-                dsub[n] = d
 
         hst = {}
 
@@ -214,7 +209,7 @@ def tile_gcnlayer_pa_t_kernel(tc, h1, adj, W2, b2, out):
                 in1=t3[:].rearrange("p (t m) -> p t m", m=4),
             )
             rx = small.tile([P, 4, 4, 32], F32, name="rx")
-            nc.vector.tensor_tensor(
+            nc.gpsimd.tensor_tensor(
                 out=rx[:],
                 in0=ra[:, :, s, :].unsqueeze(3).to_broadcast([P, 4, 4, 32]),
                 in1=sel.unsqueeze(1).unsqueeze(1).to_broadcast([P, 4, 4, 32]),
@@ -244,17 +239,26 @@ def tile_gcnlayer_pa_t_kernel(tc, h1, adj, W2, b2, out):
             y = yp.tile([P, 4, Q], BF16, name="y")
             c0 = P * g0
             c1 = P * (g1 + 1)
-            for m in range(4):
-                ri = ra[:, t, s, m : m + 1]
-                nc.vector.scalar_tensor_tensor(
-                    out=y[:, m, c0:c1], in0=raw[n][:, m, c0:c1], scalar=ri, in1=rq[:, c0:c1],
-                    op0=ALU.mult, op1=ALU.mult,
+            if g0 == 0:
+                c1 = P * s
+                d = dp.tile([P, 4, P], F32, name="d")
+                nc.gpsimd.tensor_tensor(
+                    out=d[:], in0=raw[n][:, :, c1 : c1 + P], in1=maskd[:, t, :, :], op=ALU.add
                 )
-                if g0 == 0:
-                    cd = P * s + 32 * m
+                e = dp.tile([P, 4, P], F32, name="e")
+                nc.gpsimd.tensor_tensor(
+                    out=e[:], in0=d[:],
+                    in1=rq[:, c1 : c1 + P].unsqueeze(1).to_broadcast([P, 4, P]), op=ALU.mult,
+                )
+                nc.gpsimd.tensor_tensor(
+                    out=y[:, :, c1 : c1 + P], in0=e[:],
+                    in1=ra[:, t, s, :].unsqueeze(2).to_broadcast([P, 4, P]), op=ALU.mult,
+                )
+            if c1 > c0:
+                for m in range(4):
                     nc.vector.scalar_tensor_tensor(
-                        out=y[:, m, cd : cd + 32], in0=dsub[n][:, m, :], scalar=ri,
-                        in1=rq[:, cd : cd + 32], op0=ALU.mult, op1=ALU.mult,
+                        out=y[:, m, c0:c1], in0=raw[n][:, m, c0:c1], scalar=ra[:, t, s, m : m + 1],
+                        in1=rq[:, c0:c1], op0=ALU.mult, op1=ALU.mult,
                     )
             js[n] = {"y": y}
 
@@ -320,8 +324,10 @@ def tile_gcnlayer_pa_t_kernel(tc, h1, adj, W2, b2, out):
         def stage_d(n):
             b = jobs[n][0]
             if "ob" in js[n]:
+                u = outp.tile([P, OUTF], F32, name="u")
+                nc.scalar.copy(out=u[:], in_=js[n]["ob"][:])
                 o = outp.tile([P, OUTF], F32, name="o")
-                nc.vector.tensor_tensor(out=o[:], in0=js[n]["ob"][:], in1=part[b][:], op=ALU.add)
+                nc.gpsimd.tensor_tensor(out=o[:], in0=u[:], in1=part[b][:], op=ALU.add)
                 js[n]["o"] = o
             if "o" in js[n]:
                 nc.sync.dma_start(out=out[P * b : P * b + P, :], in_=js[n]["o"][:])

@@ -29,13 +29,13 @@ def tile_gcnlayer_pa_t_kernel(tc, h1, adj, W2, b2, out):
     h1v = h1.rearrange("(t g p) k -> g p t k", t=4, g=NG)
     with ExitStack() as ctx:
         const = ctx.enter_context(tc.tile_pool(name="const", bufs=1))
-        ringp = ctx.enter_context(tc.tile_pool(name="ring", bufs=10))
+        ringp = ctx.enter_context(tc.tile_pool(name="ring", bufs=11))
         yp = ctx.enter_context(tc.tile_pool(name="y", bufs=3))
         grpp = ctx.enter_context(tc.tile_pool(name="grp", bufs=4))
         codep = ctx.enter_context(tc.tile_pool(name="code", bufs=3))
         hp = ctx.enter_context(tc.tile_pool(name="hp", bufs=2))
         small = ctx.enter_context(tc.tile_pool(name="small", bufs=2))
-        dp = ctx.enter_context(tc.tile_pool(name="diag", bufs=2))
+        dp = ctx.enter_context(tc.tile_pool(name="diag", bufs=12))
         partp = ctx.enter_context(tc.tile_pool(name="part", bufs=28))
         outp = ctx.enter_context(tc.tile_pool(name="outp", bufs=4))
         obp = ctx.enter_context(tc.psum_pool(name="ob", bufs=3))
@@ -57,10 +57,6 @@ def tile_gcnlayer_pa_t_kernel(tc, h1, adj, W2, b2, out):
             nc.vector.memset(lt[:, t, :, t], 1.0)
         sel = ident_f[:].rearrange("k (i t) -> k i t", t=4)[:, :, 0]
         dmask = ident_bf[:].rearrange("k (i t) -> k t i", t=4)
-        maskd = const.tile([P, 4, 4, P], BF16, name="maskd")
-        nc.vector.memset(maskd[:], 0.0)
-        for m in range(4):
-            nc.vector.tensor_copy(out=maskd[:, :, m, 32 * m : 32 * m + 32], in_=dmask)
         b2b = const.tile([P, OUTF], BF16, name="b2b")
         ra = const.tile([P, 4, NG, 4], F32, name="ra")
         rq = const.tile([P, Q], F32, name="rq")
@@ -86,6 +82,7 @@ def tile_gcnlayer_pa_t_kernel(tc, h1, adj, W2, b2, out):
         jobs = [(NG * t + s, 0, s) for s in range(NG) for t in range(4)]
         jobs += [(NG * t + s, s + 1, NG - 1) for s in range(NG - 1) for t in range(4)]
         raw = {}
+        dsub = {}
         h1t = {}
 
         def emit_load(n):
@@ -103,6 +100,14 @@ def tile_gcnlayer_pa_t_kernel(tc, h1, adj, W2, b2, out):
                 in_=adjq[4 * P * b : 4 * P * b + 4 * P, c0:Q].rearrange("(m k) c -> k m c", k=P),
             )
             raw[n] = rt
+            if g0 == 0:
+                d = dp.tile([P, 4, 32], F32, name="d")
+                for m in range(4):
+                    cd = P * s + 32 * m
+                    nc.gpsimd.tensor_tensor(
+                        out=d[:, m, :], in0=rt[:, m, cd : cd + 32], in1=dmask[:, b // NG, :], op=ALU.add
+                    )
+                dsub[n] = d
 
         hst = {}
 
@@ -209,7 +214,7 @@ def tile_gcnlayer_pa_t_kernel(tc, h1, adj, W2, b2, out):
                 in1=t3[:].rearrange("p (t m) -> p t m", m=4),
             )
             rx = small.tile([P, 4, 4, 32], F32, name="rx")
-            nc.gpsimd.tensor_tensor(
+            nc.vector.tensor_tensor(
                 out=rx[:],
                 in0=ra[:, :, s, :].unsqueeze(3).to_broadcast([P, 4, 4, 32]),
                 in1=sel.unsqueeze(1).unsqueeze(1).to_broadcast([P, 4, 4, 32]),
@@ -239,26 +244,17 @@ def tile_gcnlayer_pa_t_kernel(tc, h1, adj, W2, b2, out):
             y = yp.tile([P, 4, Q], BF16, name="y")
             c0 = P * g0
             c1 = P * (g1 + 1)
-            if g0 == 0:
-                c1 = P * s
-                d = dp.tile([P, 4, P], F32, name="d")
-                nc.gpsimd.tensor_tensor(
-                    out=d[:], in0=raw[n][:, :, c1 : c1 + P], in1=maskd[:, t, :, :], op=ALU.add
+            for m in range(4):
+                ri = ra[:, t, s, m : m + 1]
+                nc.vector.scalar_tensor_tensor(
+                    out=y[:, m, c0:c1], in0=raw[n][:, m, c0:c1], scalar=ri, in1=rq[:, c0:c1],
+                    op0=ALU.mult, op1=ALU.mult,
                 )
-                e = dp.tile([P, 4, P], F32, name="e")
-                nc.gpsimd.tensor_tensor(
-                    out=e[:], in0=d[:],
-                    in1=rq[:, c1 : c1 + P].unsqueeze(1).to_broadcast([P, 4, P]), op=ALU.mult,
-                )
-                nc.gpsimd.tensor_tensor(
-                    out=y[:, :, c1 : c1 + P], in0=e[:],
-                    in1=ra[:, t, s, :].unsqueeze(2).to_broadcast([P, 4, P]), op=ALU.mult,
-                )
-            if c1 > c0:
-                for m in range(4):
+                if g0 == 0:
+                    cd = P * s + 32 * m
                     nc.vector.scalar_tensor_tensor(
-                        out=y[:, m, c0:c1], in0=raw[n][:, m, c0:c1], scalar=ra[:, t, s, m : m + 1],
-                        in1=rq[:, c0:c1], op0=ALU.mult, op1=ALU.mult,
+                        out=y[:, m, cd : cd + 32], in0=dsub[n][:, m, :], scalar=ri,
+                        in1=rq[:, cd : cd + 32], op0=ALU.mult, op1=ALU.mult,
                     )
             js[n] = {"y": y}
 
@@ -324,10 +320,8 @@ def tile_gcnlayer_pa_t_kernel(tc, h1, adj, W2, b2, out):
         def stage_d(n):
             b = jobs[n][0]
             if "ob" in js[n]:
-                u = outp.tile([P, OUTF], F32, name="u")
-                nc.scalar.copy(out=u[:], in_=js[n]["ob"][:])
                 o = outp.tile([P, OUTF], F32, name="o")
-                nc.gpsimd.tensor_tensor(out=o[:], in0=u[:], in1=part[b][:], op=ALU.add)
+                nc.vector.tensor_tensor(out=o[:], in0=js[n]["ob"][:], in1=part[b][:], op=ALU.add)
                 js[n]["o"] = o
             if "o" in js[n]:
                 nc.sync.dma_start(out=out[P * b : P * b + P, :], in_=js[n]["o"][:])
@@ -372,12 +366,11 @@ def tile_gcnlayer_pa_t_kernel(tc, h1, adj, W2, b2, out):
                     h_b(n // 4 + 1)
                 if n % 4 == 2:
                     h_c(n // 4 + 1)
-            if 1 <= n <= nj:
-                stage_b(n - 1, sq)
+            if n < nj:
+                stage_b(n, sq)
             if n % 4 == 0:
                 while sq and sq[0][0] <= n // 4 + 1:
                     sum_s(*sq.pop(0))
-            if 2 <= n <= nj + 1:
-                stage_c(n - 2)
-            if n >= 3:
-                stage_d(n - 3)
+            if n < nj:
+                stage_c(n)
+                stage_d(n)

@@ -16,17 +16,21 @@ P = 128
 N = 4096
 HID = 512
 OUTF = 128
-Q = 1024
-NG = 8
-PRE = 8
-NS = [4, 6, 8, 9, 10, 11, 12, 14]
+PACK = 4
+QUARTER = N // PACK
+NG = QUARTER // P
+ROWS = P // PACK
+SUBS = P // ROWS
+SUMS = PACK * SUBS
+AHEAD = 2 * PACK
+SCALAR_SUMS = SUBS
 FLOPS = 2 * N * HID * OUTF + 2 * N * N * OUTF
 
 
 def tile_gcnlayer_pa_t_kernel(tc, h1, adj, W2, b2, out):
     nc = tc.nc
-    adjq = adj.rearrange("i (t c) -> (i t) c", t=4)
-    h1v = h1.rearrange("(t g p) k -> g p t k", t=4, g=NG)
+    adjq = adj.rearrange("i (t c) -> (i t) c", t=PACK)
+    h1v = h1.rearrange("(t g p) k -> g p t k", t=PACK, g=NG)
     with ExitStack() as ctx:
         const = ctx.enter_context(tc.tile_pool(name="const", bufs=1))
         ringp = ctx.enter_context(tc.tile_pool(name="ring", bufs=11))
@@ -45,98 +49,104 @@ def tile_gcnlayer_pa_t_kernel(tc, h1, adj, W2, b2, out):
         make_identity(nc, ident_bf[:])
         ident_f = const.tile([P, P], F32, name="ident_f")
         make_identity(nc, ident_f[:])
-        red = const.tile([P, 32], F32, name="red")
+        red = const.tile([P, ROWS], F32, name="red")
         nc.vector.tensor_reduce(
-            out=red[:], in_=ident_f[:].rearrange("k (a b) -> k a b", b=4), axis=AX.X, op=ALU.add
+            out=red[:], in_=ident_f[:].rearrange("k (a b) -> k a b", b=PACK), axis=AX.X, op=ALU.add
         )
-        b4 = const.tile([P, 32, 4], F32, name="b4")
-        nc.vector.tensor_copy(out=b4[:], in_=red[:].unsqueeze(2).to_broadcast([P, 32, 4]))
-        lt = const.tile([P, 4, 32, 4], F32, name="lt")
+        b4 = const.tile([P, ROWS, PACK], F32, name="b4")
+        nc.vector.tensor_copy(out=b4[:], in_=red[:].unsqueeze(2).to_broadcast([P, ROWS, PACK]))
+        lt = const.tile([P, PACK, ROWS, PACK], F32, name="lt")
         nc.vector.memset(lt[:], 0.0)
-        for t in range(4):
+        for t in range(PACK):
             nc.vector.memset(lt[:, t, :, t], 1.0)
-        sel = ident_f[:].rearrange("k (i t) -> k i t", t=4)[:, :, 0]
-        dmask = ident_bf[:].rearrange("k (i t) -> k t i", t=4)
+        sel = ident_f[:].rearrange("k (i t) -> k i t", t=PACK)[:, :, 0]
+        dmask = ident_bf[:].rearrange("k (i t) -> k t i", t=PACK)
         b2b = const.tile([P, OUTF], BF16, name="b2b")
-        ra = const.tile([P, 4, NG, 4], F32, name="ra")
-        rq = const.tile([P, Q], F32, name="rq")
+        ra = const.tile([P, PACK, NG, SUBS], F32, name="ra")
+        rq = const.tile([P, QUARTER], F32, name="rq")
         hcodes = [const.tile([P, OUTF], U32, name="hcodes%d" % g, align_bytes=64) for g in range(NG)]
         hscales = [const.tile([P, OUTF], U8, name="hscales%d" % g, align_bytes=64) for g in range(NG)]
         w2c = const.tile([P, OUTF], U32, name="w2c", align_bytes=64)
         w2s = const.tile([P, OUTF], U8, name="w2s", align_bytes=64)
         w2sb = const.tile([P, HID], BF16, name="w2sb")
-        w2g = const.tile([P, OUTF, 4], BF16, name="w2g", align_bytes=64)
-        junkv = const.tile([P, Q], BF16, name="junkv")
-        junks = const.tile([P, Q], BF16, name="junks")
+        w2g = const.tile([P, OUTF, PACK], BF16, name="w2g", align_bytes=64)
+        junkv = const.tile([P, QUARTER], BF16, name="junkv")
+        junks = const.tile([P, QUARTER], BF16, name="junks")
+
+        warm = const.tile([P, 2], F32, name="warm")
+        nc.vector.memset(warm[:, 0:1], 1.0)
+        nc.scalar.sqrt(out=warm[:, 1:2], in_=warm[:, 0:1])
 
         nc.sync.dma_start(out=w2sb[:], in_=W2[:, :])
         nc.sync.dma_start(out=b2b[:], in_=b2.partition_broadcast(P))
-        bankw = tp.tile([P, 4, P], BF16, name="bankw", tag="tp")
-        for t in range(4):
+        bankw = tp.tile([P, PACK, P], BF16, name="bankw", tag="tp")
+        for t in range(PACK):
             nc.tensor.transpose(bankw[:, t, :], w2sb[:, P * t : P * t + P], ident_bf[:])
         nc.scalar.copy(out=w2g[:], in_=bankw[:].rearrange("p t f -> p f t"))
         nc.vector.quantize_mx(
             out=w2c[:].bitcast(FP8X4), scales=w2s[:], in_=w2g[:].rearrange("p f t -> p (f t)")
         )
 
-        jobs = [(NG * t + s, 0, s) for s in range(NG) for t in range(4)]
-        jobs += [(NG * t + s, s + 1, NG - 1) for s in range(NG - 1) for t in range(4)]
+        jobs = [(NG * t + s, 0, s) for s in range(NG) for t in range(PACK)]
+        jobs += [(NG * t + s, s + 1, NG - 1) for s in range(NG - 1) for t in range(PACK)]
         raw = {}
-        dsub = {}
+        diag = {}
         h1t = {}
 
-        def emit_load(n):
+        def load(n):
             if n >= len(jobs):
                 return
             b, g0, g1 = jobs[n]
             s = b % NG
             if g0 == 0 and b < NG:
-                h1t[s] = hp.tile([P, 4, HID], BF16, name="h1t", bufs=3)
+                h1t[s] = hp.tile([P, PACK, HID], BF16, name="h1t", bufs=3)
                 nc.sync.dma_start(out=h1t[s][:], in_=h1v[s])
-            rt = ringp.tile([P, 4, Q], BF16, name="rt")
+            rt = ringp.tile([P, SUBS, QUARTER], BF16, name="rt")
             c0 = P * g0
             nc.sync.dma_start(
-                out=rt[:, :, c0:Q],
-                in_=adjq[4 * P * b : 4 * P * b + 4 * P, c0:Q].rearrange("(m k) c -> k m c", k=P),
+                out=rt[:, :, c0:QUARTER],
+                in_=adjq[PACK * P * b : PACK * P * b + PACK * P, c0:QUARTER].rearrange(
+                    "(m k) c -> k m c", k=P
+                ),
             )
             raw[n] = rt
             if g0 == 0:
-                d = dp.tile([P, 4, 32], F32, name="d")
-                for m in range(4):
-                    cd = P * s + 32 * m
+                d = dp.tile([P, SUBS, ROWS], F32, name="d")
+                for m in range(SUBS):
+                    cd = P * s + ROWS * m
                     nc.gpsimd.tensor_tensor(
-                        out=d[:, m, :], in0=rt[:, m, cd : cd + 32], in1=dmask[:, b // NG, :], op=ALU.add
+                        out=d[:, m, :], in0=rt[:, m, cd : cd + ROWS], in1=dmask[:, b // NG, :], op=ALU.add
                     )
-                dsub[n] = d
+                diag[n] = d
 
-        hst = {}
+        hstate = {}
 
-        def h_a(g):
-            hgrp = hp.tile([P, 512, 4], BF16, name="hgrp", align_bytes=64)
-            for hf in range(2):
-                bank = tp.tile([P, 4, 256], BF16, name="bankh", tag="tp")
+        def h_transpose(g):
+            hgrp = hp.tile([P, PACK * P, PACK], BF16, name="hgrp", align_bytes=64)
+            for half in range(2):
+                bank = tp.tile([P, PACK, 2 * P], BF16, name="bankh", tag="tp")
                 for r2 in range(2):
-                    for t in range(4):
+                    for t in range(PACK):
                         nc.tensor.transpose(
                             bank[:, t, P * r2 : P * r2 + P],
-                            h1t[g][:, 2 * hf + r2, P * t : P * t + P],
+                            h1t[g][:, 2 * half + r2, P * t : P * t + P],
                             ident_bf[:],
                         )
                 nc.scalar.copy(
-                    out=hgrp[:, 256 * hf : 256 * hf + 256, :],
+                    out=hgrp[:, 2 * P * half : 2 * P * half + 2 * P, :],
                     in_=bank[:].rearrange("p t i -> p i t"),
                 )
-            hst[g] = {"hgrp": hgrp}
+            hstate[g] = {"hgrp": hgrp}
 
-        def h_b(g):
-            hgrp = hst[g]["hgrp"]
-            hc = hp.tile([P, 512], U32, name="hc", align_bytes=64)
-            hs = hp.tile([P, 512], U8, name="hs", align_bytes=64)
+        def h_multiply(g):
+            hgrp = hstate[g]["hgrp"]
+            hc = hp.tile([P, PACK * P], U32, name="hc", align_bytes=64)
+            hs = hp.tile([P, PACK * P], U8, name="hs", align_bytes=64)
             nc.vector.quantize_mx(
                 out=hc[:].bitcast(FP8X4), scales=hs[:], in_=hgrp[:].rearrange("p i t -> p (i t)")
             )
-            hb = tp.tile([P, 4, OUTF], F32, name="hb", tag="tp")
-            for t in range(4):
+            hb = tp.tile([P, PACK, OUTF], F32, name="hb", tag="tp")
+            for t in range(PACK):
                 nc.tensor.matmul_mx(
                     out=hb[:, t, :],
                     lhsT=hc[:, P * t : P * t + P].bitcast(FP8X4),
@@ -146,15 +156,15 @@ def tile_gcnlayer_pa_t_kernel(tc, h1, adj, W2, b2, out):
                     start=True,
                     stop=True,
                 )
-            hst[g]["hb"] = hb
+            hstate[g]["hb"] = hb
 
-        def h_c(g):
-            hb = hst[g]["hb"]
-            hg = hp.tile([P, OUTF, 4], BF16, name="hg", align_bytes=64)
+        def h_quantise(g):
+            hb = hstate[g]["hb"]
+            hg = hp.tile([P, OUTF, PACK], BF16, name="hg", align_bytes=64)
             nc.vector.tensor_tensor(
                 out=hg[:],
                 in0=hb[:].rearrange("p t f -> p f t"),
-                in1=b2b[:].unsqueeze(2).to_broadcast([P, OUTF, 4]),
+                in1=b2b[:].unsqueeze(2).to_broadcast([P, OUTF, PACK]),
                 op=ALU.add,
             )
             nc.vector.quantize_mx(
@@ -163,137 +173,136 @@ def tile_gcnlayer_pa_t_kernel(tc, h1, adj, W2, b2, out):
                 in_=hg[:].rearrange("p f t -> p (f t)"),
             )
 
-        st = {}
+        rstate = {}
 
         def sums_begin(s):
-            psv = small.tile([P, 16], F32, name="psv")
-            pss = small.tile([P, 16], F32, name="pss")
-            nc.vector.memset(psv[:], 0.0)
-            nc.vector.memset(pss[:], 0.0)
-            st[s] = {"psv": psv, "pss": pss}
+            psv = small.tile([P, SUMS], F32, name="psv")
+            pss = small.tile([P, SUMS], F32, name="pss")
+            rstate[s] = {"psv": psv, "pss": pss}
 
-        def sum_v(s, i):
+        def sum_on_vector(s, u):
             nc.vector.tensor_scalar(
-                out=junkv[:], in0=raw[4 * s + i // 4][:, i % 4, :], scalar1=1.0, scalar2=None,
-                op0=ALU.mult, op1=ALU.add, accum_out=st[s]["psv"][:, i : i + 1],
+                out=junkv[:], in0=raw[PACK * s + u // SUBS][:, u % SUBS, :], scalar1=1.0, scalar2=None,
+                op0=ALU.mult, op1=ALU.add, accum_out=rstate[s]["psv"][:, u : u + 1],
             )
 
-        def sum_s(s, i):
+        def sum_on_scalar(s, u):
             nc.scalar.activation(
-                out=junks[:], in_=raw[4 * s + i // 4][:, i % 4, :], func=ACT.Copy,
-                accum_out=st[s]["pss"][:, i : i + 1],
+                out=junks[:], in_=raw[PACK * s + u // SUBS][:, u % SUBS, :], func=ACT.Copy,
+                accum_out=rstate[s]["pss"][:, u : u + 1],
             )
 
-        def r_part1(s):
-            dqp = tp.tile([P, 16], F32, name="dqp", tag="tp")
+        def r_sqrt(s):
+            dqp = tp.tile([P, SUMS], F32, name="dqp", tag="tp")
             b4v = b4[:].rearrange("k a b -> k (a b)")
-            nc.tensor.matmul(out=dqp[:], lhsT=b4v, rhs=st[s]["psv"][:], start=True, stop=False)
-            nc.tensor.matmul(out=dqp[:], lhsT=b4v, rhs=st[s]["pss"][:], start=False, stop=True)
-            deg = small.tile([P, 16], F32, name="deg")
-            nc.vector.tensor_scalar_add(out=deg[:], in0=dqp[:], scalar1=1.0)
-            sq = small.tile([P, 16], F32, name="sq")
-            nc.scalar.sqrt(out=sq[:], in_=deg[:])
-            st[s]["deg"] = deg
-            st[s]["sq"] = sq
+            nc.tensor.matmul(
+                out=dqp[:, 0:SCALAR_SUMS], lhsT=b4v, rhs=rstate[s]["pss"][:, 0:SCALAR_SUMS], start=True, stop=True
+            )
+            nc.tensor.matmul(
+                out=dqp[:, SCALAR_SUMS:SUMS], lhsT=b4v, rhs=rstate[s]["psv"][:, SCALAR_SUMS:SUMS],
+                start=True, stop=True,
+            )
+            sq = small.tile([P, SUMS], F32, name="sq")
+            nc.scalar.activation(out=sq[:], in_=dqp[:], func=ACT.Sqrt, bias=1.0)
+            rstate[s]["dqp"] = dqp
+            rstate[s]["sq"] = sq
 
-        def r_part2(s):
-            deg = st[s]["deg"]
-            r0 = small.tile([P, 16], F32, name="r0")
-            nc.vector.reciprocal(out=r0[:], in_=st[s]["sq"][:])
-            t1 = small.tile([P, 16], F32, name="t1")
+        def r_finish(s):
+            r0 = small.tile([P, SUMS], F32, name="r0")
+            nc.vector.reciprocal(out=r0[:], in_=rstate[s]["sq"][:])
+            t1 = small.tile([P, SUMS], F32, name="t1")
             nc.vector.tensor_mul(out=t1[:], in0=r0[:], in1=r0[:])
-            t2 = small.tile([P, 16], F32, name="t2")
-            nc.vector.tensor_mul(out=t2[:], in0=t1[:], in1=deg[:])
-            t3 = small.tile([P, 16], F32, name="t3")
+            t2 = small.tile([P, SUMS], F32, name="t2")
+            nc.vector.scalar_tensor_tensor(
+                out=t2[:], in0=rstate[s]["dqp"][:], scalar=1.0, in1=t1[:], op0=ALU.add, op1=ALU.mult
+            )
+            t3 = small.tile([P, SUMS], F32, name="t3")
             nc.vector.tensor_scalar(
                 out=t3[:], in0=t2[:], scalar1=-0.5, scalar2=1.5, op0=ALU.mult, op1=ALU.add
             )
             nc.vector.tensor_mul(
                 out=ra[:, :, s, :],
-                in0=r0[:].rearrange("p (t m) -> p t m", m=4),
-                in1=t3[:].rearrange("p (t m) -> p t m", m=4),
+                in0=r0[:].rearrange("p (t m) -> p t m", m=SUBS),
+                in1=t3[:].rearrange("p (t m) -> p t m", m=SUBS),
             )
-            rx = small.tile([P, 4, 4, 32], F32, name="rx")
+            rx = small.tile([P, PACK, SUBS, ROWS], F32, name="rx")
             nc.vector.tensor_tensor(
                 out=rx[:],
-                in0=ra[:, :, s, :].unsqueeze(3).to_broadcast([P, 4, 4, 32]),
-                in1=sel.unsqueeze(1).unsqueeze(1).to_broadcast([P, 4, 4, 32]),
+                in0=ra[:, :, s, :].unsqueeze(3).to_broadcast([P, PACK, SUBS, ROWS]),
+                in1=sel.unsqueeze(1).unsqueeze(1).to_broadcast([P, PACK, SUBS, ROWS]),
                 op=ALU.mult,
             )
             bq = tp.tile([P, P], F32, name="bq", tag="tp")
-            for t in range(4):
+            for t in range(PACK):
                 nc.tensor.matmul(
                     out=bq[:],
                     lhsT=lt[:, t, :, :].rearrange("k a b -> k (a b)"),
                     rhs=rx[:, t, :, :].rearrange("k m i -> k (m i)"),
                     start=(t == 0),
-                    stop=(t == 3),
+                    stop=(t == PACK - 1),
                 )
-            st[s]["bq"] = bq
+            rstate[s]["bq"] = bq
 
-        def r_part3(s):
-            nc.vector.tensor_copy(out=rq[:, P * s : P * s + P], in_=st[s]["bq"][:])
+        def r_table(s):
+            nc.scalar.copy(out=rq[:, P * s : P * s + P], in_=rstate[s]["bq"][:])
 
-        js = {}
         part = {}
 
-        def stage_a(n):
+        def scale(n):
             b, g0, g1 = jobs[n]
             s = b % NG
             t = b // NG
-            y = yp.tile([P, 4, Q], BF16, name="y")
+            y = yp.tile([P, SUBS, QUARTER], BF16, name="y")
             c0 = P * g0
             c1 = P * (g1 + 1)
-            for m in range(4):
+            for m in range(SUBS):
                 ri = ra[:, t, s, m : m + 1]
                 nc.vector.scalar_tensor_tensor(
                     out=y[:, m, c0:c1], in0=raw[n][:, m, c0:c1], scalar=ri, in1=rq[:, c0:c1],
                     op0=ALU.mult, op1=ALU.mult,
                 )
                 if g0 == 0:
-                    cd = P * s + 32 * m
+                    cd = P * s + ROWS * m
                     nc.vector.scalar_tensor_tensor(
-                        out=y[:, m, cd : cd + 32], in0=dsub[n][:, m, :], scalar=ri,
-                        in1=rq[:, cd : cd + 32], op0=ALU.mult, op1=ALU.mult,
+                        out=y[:, m, cd : cd + ROWS], in0=diag[n][:, m, :], scalar=ri,
+                        in1=rq[:, cd : cd + ROWS], op0=ALU.mult, op1=ALU.mult,
                     )
-            js[n] = {"y": y}
+            return y
 
-        def stage_b(n, sq):
+        def transpose(n, y, waiting_sums):
             b, g0, g1 = jobs[n]
-            y = js[n]["y"]
-            grp = grpp.tile([P, NG, 512], BF16, name="grp", align_bytes=64)
+            grp = grpp.tile([P, NG, PACK * P], BF16, name="grp", align_bytes=64)
             g = g0
             while g <= g1:
-                k = min(2, g1 - g + 1)
-                bank = tp.tile([P, 2, 512], BF16, name="bank", tag="tp")
-                for gl in range(k):
-                    for m in range(4):
+                npass = min(2, g1 - g + 1)
+                bank = tp.tile([P, 2, PACK * P], BF16, name="bank", tag="tp")
+                for gl in range(npass):
+                    for m in range(SUBS):
                         c = P * (g + gl)
                         nc.tensor.transpose(
                             bank[:, gl, P * m : P * m + P], y[:, m, c : c + P], ident_bf[:]
                         )
-                nc.scalar.copy(out=grp[:, g : g + k, :], in_=bank[:, 0:k, :])
-                if sq:
-                    sum_s(*sq.pop(0))
-                g += k
-            js[n]["grp"] = grp
+                nc.scalar.copy(out=grp[:, g : g + npass, :], in_=bank[:, 0:npass, :])
+                if waiting_sums:
+                    sum_on_scalar(*waiting_sums.pop(0))
+                g += npass
+            return grp
 
-        def stage_c(n):
+        def multiply(n, grp):
             b, g0, g1 = jobs[n]
-            grp = js[n]["grp"]
             codes = codep.tile([P, NG, P], U32, name="codes", align_bytes=64)
             scl = codep.tile([P, NG, P], U8, name="scl", align_bytes=64)
             g = g0
             while g <= g1:
-                k = 1
-                while 2 * k <= g1 - g + 1:
-                    k = 2 * k
+                npass = 1
+                while 2 * npass <= g1 - g + 1:
+                    npass = 2 * npass
                 nc.vector.quantize_mx(
-                    out=codes[:, g : g + k, :].rearrange("p g i -> p (g i)").bitcast(FP8X4),
-                    scales=scl[:, g : g + k, :].rearrange("p g i -> p (g i)"),
-                    in_=grp[:, g : g + k, :].rearrange("p g i -> p (g i)"),
+                    out=codes[:, g : g + npass, :].rearrange("p g i -> p (g i)").bitcast(FP8X4),
+                    scales=scl[:, g : g + npass, :].rearrange("p g i -> p (g i)"),
+                    in_=grp[:, g : g + npass, :].rearrange("p g i -> p (g i)"),
                 )
-                g += k
+                g += npass
             ob = obp.tile([P, OUTF], F32, name="ob")
             for g in range(g0, g1 + 1):
                 nc.tensor.matmul_mx(
@@ -309,68 +318,54 @@ def tile_gcnlayer_pa_t_kernel(tc, h1, adj, W2, b2, out):
                 pt = partp.tile([P, OUTF], F32, name="pt")
                 nc.scalar.copy(out=pt[:], in_=ob[:])
                 part[b] = pt
+                return
+            o = outp.tile([P, OUTF], F32, name="o")
+            if g0 == 0:
+                nc.scalar.copy(out=o[:], in_=ob[:])
             else:
-                if g0 == 0:
-                    o = outp.tile([P, OUTF], F32, name="o")
-                    nc.scalar.copy(out=o[:], in_=ob[:])
-                    js[n]["o"] = o
-                else:
-                    js[n]["ob"] = ob
+                nc.vector.tensor_tensor(out=o[:], in0=ob[:], in1=part[b][:], op=ALU.add)
+            nc.sync.dma_start(out=out[P * b : P * b + P, :], in_=o[:])
 
-        def stage_d(n):
-            b = jobs[n][0]
-            if "ob" in js[n]:
-                o = outp.tile([P, OUTF], F32, name="o")
-                nc.vector.tensor_tensor(out=o[:], in0=js[n]["ob"][:], in1=part[b][:], op=ALU.add)
-                js[n]["o"] = o
-            if "o" in js[n]:
-                nc.sync.dma_start(out=out[P * b : P * b + P, :], in_=js[n]["o"][:])
-
-        for n in range(PRE):
-            emit_load(n)
+        for n in range(AHEAD):
+            load(n)
         sums_begin(0)
-        for i in range(16):
-            if i % 4 < 3:
-                sum_v(0, i)
+        for u in range(SUMS):
+            if u >= SCALAR_SUMS:
+                sum_on_vector(0, u)
             else:
-                sum_s(0, i)
-        r_part1(0)
-        r_part2(0)
-        r_part3(0)
-        h_a(0)
-        h_b(0)
-        h_c(0)
-        sq = []
-        nj = len(jobs)
-        for n in range(nj + 3):
+                sum_on_scalar(0, u)
+        r_sqrt(0)
+        r_finish(0)
+        r_table(0)
+        h_transpose(0)
+        h_multiply(0)
+        h_quantise(0)
+        waiting_sums = []
+        for n in range(len(jobs)):
             for q in range(1, NG):
-                if n == max(0, 4 * q - 7):
+                if n == max(0, PACK * q - 7):
                     sums_begin(q)
-                    sq.extend([(q, i) for i in range(NS[q])])
-                if n == 4 * q - 4:
-                    for i in range(NS[q], 16):
-                        sum_v(q, i)
-                if n == 4 * q - 3:
-                    r_part1(q)
-                if n == 4 * q - 2:
-                    r_part2(q)
-                if n == 4 * q - 1:
-                    r_part3(q)
-            if n < nj:
-                stage_a(n)
-                emit_load(n + PRE)
-            if n // 4 + 1 < NG:
-                if n % 4 == 0:
-                    h_a(n // 4 + 1)
-                if n % 4 == 1:
-                    h_b(n // 4 + 1)
-                if n % 4 == 2:
-                    h_c(n // 4 + 1)
-            if n < nj:
-                stage_b(n, sq)
-            if n % 4 == 0:
-                while sq and sq[0][0] <= n // 4 + 1:
-                    sum_s(*sq.pop(0))
-            if n < nj:
-                stage_c(n)
-                stage_d(n)
+                    waiting_sums.extend([(q, u) for u in range(SCALAR_SUMS)])
+                if n == PACK * q - 4:
+                    for u in range(SCALAR_SUMS, SUMS):
+                        sum_on_vector(q, u)
+                if n == PACK * q - 3:
+                    r_sqrt(q)
+                if n == PACK * q - 2:
+                    r_finish(q)
+                if n == PACK * q - 1:
+                    r_table(q)
+            y = scale(n)
+            load(n + AHEAD)
+            if n // PACK + 1 < NG:
+                if n % PACK == 0:
+                    h_transpose(n // PACK + 1)
+                if n % PACK == 1:
+                    h_multiply(n // PACK + 1)
+                if n % PACK == 2:
+                    h_quantise(n // PACK + 1)
+            grp = transpose(n, y, waiting_sums)
+            if n % PACK == 0:
+                while waiting_sums and waiting_sums[0][0] <= n // PACK + 1:
+                    sum_on_scalar(*waiting_sums.pop(0))
+            multiply(n, grp)

@@ -23,7 +23,7 @@ ROWS = P // PACK
 SUBS = P // ROWS
 SUMS = PACK * SUBS
 AHEAD = 2 * PACK
-SCALAR_SUMS = SUBS
+SCALAR_SUMS = [4, 4, 6, 6, 6, 8, 8, 8]
 FLOPS = 2 * N * HID * OUTF + 2 * N * N * OUTF
 
 
@@ -195,12 +195,12 @@ def tile_gcnlayer_pa_t_kernel(tc, h1, adj, W2, b2, out):
         def r_sqrt(s):
             dqp = tp.tile([P, SUMS], F32, name="dqp", tag="tp")
             b4v = b4[:].rearrange("k a b -> k (a b)")
+            split = SCALAR_SUMS[s]
             nc.tensor.matmul(
-                out=dqp[:, 0:SCALAR_SUMS], lhsT=b4v, rhs=rstate[s]["pss"][:, 0:SCALAR_SUMS], start=True, stop=True
+                out=dqp[:, 0:split], lhsT=b4v, rhs=rstate[s]["pss"][:, 0:split], start=True, stop=True
             )
             nc.tensor.matmul(
-                out=dqp[:, SCALAR_SUMS:SUMS], lhsT=b4v, rhs=rstate[s]["psv"][:, SCALAR_SUMS:SUMS],
-                start=True, stop=True,
+                out=dqp[:, split:SUMS], lhsT=b4v, rhs=rstate[s]["psv"][:, split:SUMS], start=True, stop=True
             )
             sq = small.tile([P, SUMS], F32, name="sq")
             nc.scalar.activation(out=sq[:], in_=dqp[:], func=ACT.Sqrt, bias=1.0)
@@ -330,7 +330,7 @@ def tile_gcnlayer_pa_t_kernel(tc, h1, adj, W2, b2, out):
             load(n)
         sums_begin(0)
         for u in range(SUMS):
-            if u >= SCALAR_SUMS:
+            if u >= SCALAR_SUMS[0]:
                 sum_on_vector(0, u)
             else:
                 sum_on_scalar(0, u)
@@ -345,9 +345,9 @@ def tile_gcnlayer_pa_t_kernel(tc, h1, adj, W2, b2, out):
             for q in range(1, NG):
                 if n == max(0, PACK * q - 7):
                     sums_begin(q)
-                    waiting_sums.extend([(q, u) for u in range(SCALAR_SUMS)])
+                    waiting_sums.extend([(q, u) for u in range(SCALAR_SUMS[q])])
                 if n == PACK * q - 4:
-                    for u in range(SCALAR_SUMS, SUMS):
+                    for u in range(SCALAR_SUMS[q], SUMS):
                         sum_on_vector(q, u)
                 if n == PACK * q - 3:
                     r_sqrt(q)

from contextlib import ExitStack

import concourse.mybir as mybir
from concourse.masks import make_identity

F32 = mybir.dt.float32
BF16 = mybir.dt.bfloat16
U32 = mybir.dt.uint32
U8 = mybir.dt.uint8
FP8X4 = mybir.dt.float8_e4m3fn_x4
ALU = mybir.AluOpType
ACT = mybir.ActivationFunctionType
AX = mybir.AxisListType

P = 128
N = 4096
HID = 512
OUTF = 128
PACK = 4
QUARTER = N // PACK
NG = QUARTER // P
ROWS = P // PACK
SUBS = P // ROWS
SUMS = PACK * SUBS
AHEAD = 2 * PACK
SCALAR_SUMS = [4, 4, 6, 6, 6, 8, 8, 8]
FLOPS = 2 * N * HID * OUTF + 2 * N * N * OUTF


def tile_gcnlayer_pa_t_kernel(tc, h1, adj, W2, b2, out):
    nc = tc.nc
    adjq = adj.rearrange("i (t c) -> (i t) c", t=PACK)
    h1v = h1.rearrange("(t g p) k -> g p t k", t=PACK, g=NG)
    with ExitStack() as ctx:
        const = ctx.enter_context(tc.tile_pool(name="const", bufs=1))
        ringp = ctx.enter_context(tc.tile_pool(name="ring", bufs=11))
        yp = ctx.enter_context(tc.tile_pool(name="y", bufs=3))
        grpp = ctx.enter_context(tc.tile_pool(name="grp", bufs=4))
        codep = ctx.enter_context(tc.tile_pool(name="code", bufs=3))
        hp = ctx.enter_context(tc.tile_pool(name="hp", bufs=2))
        small = ctx.enter_context(tc.tile_pool(name="small", bufs=2))
        dp = ctx.enter_context(tc.tile_pool(name="diag", bufs=12))
        partp = ctx.enter_context(tc.tile_pool(name="part", bufs=28))
        outp = ctx.enter_context(tc.tile_pool(name="outp", bufs=4))
        obp = ctx.enter_context(tc.psum_pool(name="ob", bufs=3))
        tp = ctx.enter_context(tc.psum_pool(name="tp", bufs=5))

        ident_bf = const.tile([P, P], BF16, name="ident_bf")
        make_identity(nc, ident_bf[:])
        ident_f = const.tile([P, P], F32, name="ident_f")
        make_identity(nc, ident_f[:])
        red = const.tile([P, ROWS], F32, name="red")
        nc.vector.tensor_reduce(
            out=red[:], in_=ident_f[:].rearrange("k (a b) -> k a b", b=PACK), axis=AX.X, op=ALU.add
        )
        b4 = const.tile([P, ROWS, PACK], F32, name="b4")
        nc.vector.tensor_copy(out=b4[:], in_=red[:].unsqueeze(2).to_broadcast([P, ROWS, PACK]))
        lt = const.tile([P, PACK, ROWS, PACK], F32, name="lt")
        nc.vector.memset(lt[:], 0.0)
        for t in range(PACK):
            nc.vector.memset(lt[:, t, :, t], 1.0)
        sel = ident_f[:].rearrange("k (i t) -> k i t", t=PACK)[:, :, 0]
        dmask = ident_bf[:].rearrange("k (i t) -> k t i", t=PACK)
        b2b = const.tile([P, OUTF], BF16, name="b2b")
        ra = const.tile([P, PACK, NG, SUBS], F32, name="ra")
        rq = const.tile([P, QUARTER], F32, name="rq")
        hcodes = [const.tile([P, OUTF], U32, name="hcodes%d" % g, align_bytes=64) for g in range(NG)]
        hscales = [const.tile([P, OUTF], U8, name="hscales%d" % g, align_bytes=64) for g in range(NG)]
        w2c = const.tile([P, OUTF], U32, name="w2c", align_bytes=64)
        w2s = const.tile([P, OUTF], U8, name="w2s", align_bytes=64)
        w2sb = const.tile([P, HID], BF16, name="w2sb")
        w2g = const.tile([P, OUTF, PACK], BF16, name="w2g", align_bytes=64)
        junkv = const.tile([P, QUARTER], BF16, name="junkv")
        junks = const.tile([P, QUARTER], BF16, name="junks")

        warm = const.tile([P, 2], F32, name="warm")
        nc.vector.memset(warm[:, 0:1], 1.0)
        nc.scalar.sqrt(out=warm[:, 1:2], in_=warm[:, 0:1])

        nc.sync.dma_start(out=w2sb[:], in_=W2[:, :])
        nc.sync.dma_start(out=b2b[:], in_=b2.partition_broadcast(P))
        bankw = tp.tile([P, PACK, P], BF16, name="bankw", tag="tp")
        for t in range(PACK):
            nc.tensor.transpose(bankw[:, t, :], w2sb[:, P * t : P * t + P], ident_bf[:])
        nc.scalar.copy(out=w2g[:], in_=bankw[:].rearrange("p t f -> p f t"))
        nc.vector.quantize_mx(
            out=w2c[:].bitcast(FP8X4), scales=w2s[:], in_=w2g[:].rearrange("p f t -> p (f t)")
        )

        jobs = [(NG * t + s, 0, s) for s in range(NG) for t in range(PACK)]
        jobs += [(NG * t + s, s + 1, NG - 1) for s in range(NG - 1) for t in range(PACK)]
        raw = {}
        diag = {}
        h1t = {}

        def load(n):
            if n >= len(jobs):
                return
            b, g0, g1 = jobs[n]
            s = b % NG
            if g0 == 0 and b < NG:
                h1t[s] = hp.tile([P, PACK, HID], BF16, name="h1t", bufs=3)
                nc.sync.dma_start(out=h1t[s][:], in_=h1v[s])
            rt = ringp.tile([P, SUBS, QUARTER], BF16, name="rt")
            c0 = P * g0
            nc.sync.dma_start(
                out=rt[:, :, c0:QUARTER],
                in_=adjq[PACK * P * b : PACK * P * b + PACK * P, c0:QUARTER].rearrange(
                    "(m k) c -> k m c", k=P
                ),
            )
            raw[n] = rt
            if g0 == 0:
                d = dp.tile([P, SUBS, ROWS], F32, name="d")
                for m in range(SUBS):
                    cd = P * s + ROWS * m
                    nc.gpsimd.tensor_tensor(
                        out=d[:, m, :], in0=rt[:, m, cd : cd + ROWS], in1=dmask[:, b // NG, :], op=ALU.add
                    )
                diag[n] = d

        hstate = {}

        def h_transpose(g):
            hgrp = hp.tile([P, PACK * P, PACK], BF16, name="hgrp", align_bytes=64)
            for half in range(2):
                bank = tp.tile([P, PACK, 2 * P], BF16, name="bankh", tag="tp")
                for r2 in range(2):
                    for t in range(PACK):
                        nc.tensor.transpose(
                            bank[:, t, P * r2 : P * r2 + P],
                            h1t[g][:, 2 * half + r2, P * t : P * t + P],
                            ident_bf[:],
                        )
                nc.scalar.copy(
                    out=hgrp[:, 2 * P * half : 2 * P * half + 2 * P, :],
                    in_=bank[:].rearrange("p t i -> p i t"),
                )
            hstate[g] = {"hgrp": hgrp}

        def h_multiply(g):
            hgrp = hstate[g]["hgrp"]
            hc = hp.tile([P, PACK * P], U32, name="hc", align_bytes=64)
            hs = hp.tile([P, PACK * P], U8, name="hs", align_bytes=64)
            nc.vector.quantize_mx(
                out=hc[:].bitcast(FP8X4), scales=hs[:], in_=hgrp[:].rearrange("p i t -> p (i t)")
            )
            hb = tp.tile([P, PACK, OUTF], F32, name="hb", tag="tp")
            for t in range(PACK):
                nc.tensor.matmul_mx(
                    out=hb[:, t, :],
                    lhsT=hc[:, P * t : P * t + P].bitcast(FP8X4),
                    lhsT_scale=hs[:, P * t : P * t + P],
                    rhs=w2c[:].bitcast(FP8X4),
                    rhs_scale=w2s[:],
                    start=True,
                    stop=True,
                )
            hstate[g]["hb"] = hb

        def h_quantise(g):
            hb = hstate[g]["hb"]
            hg = hp.tile([P, OUTF, PACK], BF16, name="hg", align_bytes=64)
            nc.vector.tensor_tensor(
                out=hg[:],
                in0=hb[:].rearrange("p t f -> p f t"),
                in1=b2b[:].unsqueeze(2).to_broadcast([P, OUTF, PACK]),
                op=ALU.add,
            )
            nc.vector.quantize_mx(
                out=hcodes[g][:].bitcast(FP8X4),
                scales=hscales[g][:],
                in_=hg[:].rearrange("p f t -> p (f t)"),
            )

        rstate = {}

        def sums_begin(s):
            psv = small.tile([P, SUMS], F32, name="psv")
            pss = small.tile([P, SUMS], F32, name="pss")
            rstate[s] = {"psv": psv, "pss": pss}

        def sum_on_vector(s, u):
            nc.vector.tensor_scalar(
                out=junkv[:], in0=raw[PACK * s + u // SUBS][:, u % SUBS, :], scalar1=1.0, scalar2=None,
                op0=ALU.mult, op1=ALU.add, accum_out=rstate[s]["psv"][:, u : u + 1],
            )

        def sum_on_scalar(s, u):
            nc.scalar.activation(
                out=junks[:], in_=raw[PACK * s + u // SUBS][:, u % SUBS, :], func=ACT.Copy,
                accum_out=rstate[s]["pss"][:, u : u + 1],
            )

        def r_sqrt(s):
            dqp = tp.tile([P, SUMS], F32, name="dqp", tag="tp")
            b4v = b4[:].rearrange("k a b -> k (a b)")
            split = SCALAR_SUMS[s]
            nc.tensor.matmul(
                out=dqp[:, 0:split], lhsT=b4v, rhs=rstate[s]["pss"][:, 0:split], start=True, stop=True
            )
            nc.tensor.matmul(
                out=dqp[:, split:SUMS], lhsT=b4v, rhs=rstate[s]["psv"][:, split:SUMS], start=True, stop=True
            )
            sq = small.tile([P, SUMS], F32, name="sq")
            nc.scalar.activation(out=sq[:], in_=dqp[:], func=ACT.Sqrt, bias=1.0)
            rstate[s]["dqp"] = dqp
            rstate[s]["sq"] = sq

        def r_finish(s):
            r0 = small.tile([P, SUMS], F32, name="r0")
            nc.vector.reciprocal(out=r0[:], in_=rstate[s]["sq"][:])
            t1 = small.tile([P, SUMS], F32, name="t1")
            nc.vector.tensor_mul(out=t1[:], in0=r0[:], in1=r0[:])
            t2 = small.tile([P, SUMS], F32, name="t2")
            nc.vector.scalar_tensor_tensor(
                out=t2[:], in0=rstate[s]["dqp"][:], scalar=1.0, in1=t1[:], op0=ALU.add, op1=ALU.mult
            )
            t3 = small.tile([P, SUMS], F32, name="t3")
            nc.vector.tensor_scalar(
                out=t3[:], in0=t2[:], scalar1=-0.5, scalar2=1.5, op0=ALU.mult, op1=ALU.add
            )
            nc.vector.tensor_mul(
                out=ra[:, :, s, :],
                in0=r0[:].rearrange("p (t m) -> p t m", m=SUBS),
                in1=t3[:].rearrange("p (t m) -> p t m", m=SUBS),
            )
            rx = small.tile([P, PACK, SUBS, ROWS], F32, name="rx")
            nc.vector.tensor_tensor(
                out=rx[:],
                in0=ra[:, :, s, :].unsqueeze(3).to_broadcast([P, PACK, SUBS, ROWS]),
                in1=sel.unsqueeze(1).unsqueeze(1).to_broadcast([P, PACK, SUBS, ROWS]),
                op=ALU.mult,
            )
            bq = tp.tile([P, P], F32, name="bq", tag="tp")
            for t in range(PACK):
                nc.tensor.matmul(
                    out=bq[:],
                    lhsT=lt[:, t, :, :].rearrange("k a b -> k (a b)"),
                    rhs=rx[:, t, :, :].rearrange("k m i -> k (m i)"),
                    start=(t == 0),
                    stop=(t == PACK - 1),
                )
            rstate[s]["bq"] = bq

        def r_table(s):
            nc.scalar.copy(out=rq[:, P * s : P * s + P], in_=rstate[s]["bq"][:])

        part = {}

        def scale(n):
            b, g0, g1 = jobs[n]
            s = b % NG
            t = b // NG
            y = yp.tile([P, SUBS, QUARTER], BF16, name="y")
            c0 = P * g0
            c1 = P * (g1 + 1)
            for m in range(SUBS):
                ri = ra[:, t, s, m : m + 1]
                nc.vector.scalar_tensor_tensor(
                    out=y[:, m, c0:c1], in0=raw[n][:, m, c0:c1], scalar=ri, in1=rq[:, c0:c1],
                    op0=ALU.mult, op1=ALU.mult,
                )
                if g0 == 0:
                    cd = P * s + ROWS * m
                    nc.vector.scalar_tensor_tensor(
                        out=y[:, m, cd : cd + ROWS], in0=diag[n][:, m, :], scalar=ri,
                        in1=rq[:, cd : cd + ROWS], op0=ALU.mult, op1=ALU.mult,
                    )
            return y

        def transpose(n, y, waiting_sums):
            b, g0, g1 = jobs[n]
            grp = grpp.tile([P, NG, PACK * P], BF16, name="grp", align_bytes=64)
            g = g0
            while g <= g1:
                npass = min(2, g1 - g + 1)
                bank = tp.tile([P, 2, PACK * P], BF16, name="bank", tag="tp")
                for gl in range(npass):
                    for m in range(SUBS):
                        c = P * (g + gl)
                        nc.tensor.transpose(
                            bank[:, gl, P * m : P * m + P], y[:, m, c : c + P], ident_bf[:]
                        )
                nc.scalar.copy(out=grp[:, g : g + npass, :], in_=bank[:, 0:npass, :])
                if waiting_sums:
                    sum_on_scalar(*waiting_sums.pop(0))
                g += npass
            return grp

        def multiply(n, grp):
            b, g0, g1 = jobs[n]
            codes = codep.tile([P, NG, P], U32, name="codes", align_bytes=64)
            scl = codep.tile([P, NG, P], U8, name="scl", align_bytes=64)
            g = g0
            while g <= g1:
                npass = 1
                while 2 * npass <= g1 - g + 1:
                    npass = 2 * npass
                nc.vector.quantize_mx(
                    out=codes[:, g : g + npass, :].rearrange("p g i -> p (g i)").bitcast(FP8X4),
                    scales=scl[:, g : g + npass, :].rearrange("p g i -> p (g i)"),
                    in_=grp[:, g : g + npass, :].rearrange("p g i -> p (g i)"),
                )
                g += npass
            ob = obp.tile([P, OUTF], F32, name="ob")
            for g in range(g0, g1 + 1):
                nc.tensor.matmul_mx(
                    out=ob[:],
                    lhsT=codes[:, g, :].bitcast(FP8X4),
                    lhsT_scale=scl[:, g, :],
                    rhs=hcodes[g][:].bitcast(FP8X4),
                    rhs_scale=hscales[g][:],
                    start=(g == g0),
                    stop=(g == g1),
                )
            if g1 < NG - 1:
                pt = partp.tile([P, OUTF], F32, name="pt")
                nc.scalar.copy(out=pt[:], in_=ob[:])
                part[b] = pt
                return
            o = outp.tile([P, OUTF], F32, name="o")
            if g0 == 0:
                nc.scalar.copy(out=o[:], in_=ob[:])
            else:
                nc.vector.tensor_tensor(out=o[:], in0=ob[:], in1=part[b][:], op=ALU.add)
            nc.sync.dma_start(out=out[P * b : P * b + P, :], in_=o[:])

        for n in range(AHEAD):
            load(n)
        sums_begin(0)
        for u in range(SUMS):
            if u >= SCALAR_SUMS[0]:
                sum_on_vector(0, u)
            else:
                sum_on_scalar(0, u)
        r_sqrt(0)
        r_finish(0)
        r_table(0)
        h_transpose(0)
        h_multiply(0)
        h_quantise(0)
        waiting_sums = []
        for n in range(len(jobs)):
            for q in range(1, NG):
                if n == max(0, PACK * q - 7):
                    sums_begin(q)
                    waiting_sums.extend([(q, u) for u in range(SCALAR_SUMS[q])])
                if n == PACK * q - 4:
                    for u in range(SCALAR_SUMS[q], SUMS):
                        sum_on_vector(q, u)
                if n == PACK * q - 3:
                    r_sqrt(q)
                if n == PACK * q - 2:
                    r_finish(q)
                if n == PACK * q - 1:
                    r_table(q)
            y = scale(n)
            load(n + AHEAD)
            if n // PACK + 1 < NG:
                if n % PACK == 0:
                    h_transpose(n // PACK + 1)
                if n % PACK == 1:
                    h_multiply(n // PACK + 1)
                if n % PACK == 2:
                    h_quantise(n // PACK + 1)
            grp = transpose(n, y, waiting_sums)
            if n % PACK == 0:
                while waiting_sums and waiting_sums[0][0] <= n // PACK + 1:
                    sum_on_scalar(*waiting_sums.pop(0))
            multiply(n, grp)
